import numpy as np
import ml_dtypes


def mxq(x, axis, fmt="e4m3"):
    dtype, down = {"e4m3": (ml_dtypes.float8_e4m3fn, 7), "e5m2": (ml_dtypes.float8_e5m2, 14)}[fmt]
    v = np.moveaxis(np.asarray(x, np.float32).astype(ml_dtypes.bfloat16).astype(np.float64), axis, -1)
    blocks = v.reshape(v.shape[:-1] + (-1, 32))
    amax = np.abs(blocks).max(-1, keepdims=True)
    byte = np.maximum(np.where(amax > 0, np.frexp(amax)[1] - 1 + 127, 0) - down, 1)
    scale = np.exp2(byte - 127.0)
    codes = (blocks / scale).astype(np.float32).astype(dtype).astype(np.float64)
    return np.moveaxis((codes * scale).reshape(v.shape), -1, axis)


WIDE = False


def mx_kscale(k):
    if not WIDE:
        return np.ones(k)
    levels = np.array([20, -20, 10, -10, 0])
    a = np.random.permutation(np.resize(levels, k // 512 * 4)).reshape(k // 512, 4)
    idx = np.arange(k)
    return np.exp2(a[idx // 512, idx % 128 // 32])


BF16 = ml_dtypes.bfloat16


def bf(x):
    return np.asarray(x, np.float32).astype(BF16)


def f64(x):
    return np.asarray(x).astype(np.float64)


B, S, D_IN, D_OUT = 3, 512, 1024, 1024
T = B * S


def relative_shift(x):
    b, s, d = x.shape
    padded = np.concatenate([np.zeros((b, 1, d)), x], axis=1).reshape(s + 1, b, d)
    return padded[1:].reshape(b, s, d)


def setup_inputs():
    sv = mx_kscale(T)
    idx = (S + 1) * np.arange(B)[:, None] + np.arange(S)[None, :] + 1 - B
    fac = np.where(idx >= 0, sv[np.maximum(idx, 0)], 1.0)[:, :, None]
    pos_embed = np.random.standard_normal((B, S, D_IN)) * fac
    W_r = np.random.standard_normal((D_OUT, D_IN)) * 1.2 / np.sqrt(D_IN)
    b_r = np.random.standard_normal(D_OUT) * 0.3
    g = np.random.standard_normal((B, S, D_OUT)) * np.exp2(np.random.randint(-12, 1, (B, S, 1))) / sv.reshape(B, S, 1)
    return {"pos_embed": bf(pos_embed), "W_r": bf(W_r), "b_r": bf(b_r), "grad_out": bf(g)}


def reference(pos_embed, W_r, b_r, grad_out):
    shifted = relative_shift(f64(pos_embed)).reshape(T, D_IN)
    g = f64(grad_out).reshape(T, D_OUT)
    return mxq(g, 0, "e5m2").T @ mxq(shifted, 0, "e4m3")

@@ -1,0 +1,181 @@
+from contextlib import ExitStack
+
+import concourse.mybir as mybir
+
+BF16 = mybir.dt.bfloat16
+F32 = mybir.dt.float32
+U32 = mybir.dt.uint32
+U8 = mybir.dt.uint8
+E4M3_X4 = mybir.dt.float8_e4m3fn_x4
+E5M2_X4 = mybir.dt.float8_e5m2_x4
+
+P = 128
+PACK = 4
+K_PASS = P * PACK
+BLOCK_PARTITIONS = 8
+
+TOKENS = 1536
+D_OUT = 1024
+D_IN = 1024
+PASSES = TOKENS // K_PASS
+
+M_TILE = 128
+N_TILE = 512
+ROUNDS = 2
+ROUND_ROWS = D_OUT // ROUNDS
+M_TILES = ROUND_ROWS // M_TILE
+N_TILES = D_IN // N_TILE
+
+UNIT = 512
+RUN = 4
+VECTOR_COLS = UNIT // 2
+GROUPED_BUFS = 4
+
+PASS_ORDER = (2, 1, 0)
+
+FLOPS = 2 * TOKENS * D_OUT * D_IN
+BYTES = 2 * (TOKENS - 2) * D_IN + 2 * TOKENS * D_OUT + 4 * D_OUT * D_IN
+
+
+def tile_relativemultiheadattention_pa_kernel(tc, pos_embed, W_r, b_r, grad_out, out):
+    nc = tc.nc
+    pos = pos_embed.flatten_outer_dims()
+    grad = grad_out.flatten_outer_dims()
+
+    with ExitStack() as stack:
+        raw_pool = stack.enter_context(tc.tile_pool(name="raw", bufs=1))
+        grouped_pool = stack.enter_context(tc.tile_pool(name="grouped", bufs=GROUPED_BUFS))
+        mx_pool = stack.enter_context(tc.tile_pool(name="mx", bufs=1))
+        result_pool = stack.enter_context(tc.tile_pool(name="result", bufs=ROUNDS * M_TILES * N_TILES))
+        psum_pool = stack.enter_context(tc.psum_pool(name="psum", bufs=M_TILES * N_TILES))
+
+        raw_x = [raw_pool.tile([P, PACK, D_IN], BF16, name="raw_x%d" % c) for c in range(PASSES)]
+        raw_g = [
+            [raw_pool.tile([P, PACK, ROUND_ROWS], BF16, name="raw_g%d_%d" % (c, r)) for r in range(ROUNDS)]
+            for c in range(PASSES)
+        ]
+        x_codes = mx_pool.tile([P, PASSES, D_IN], U32, name="x_codes", align_bytes=64)
+        x_scales = mx_pool.tile([P, PASSES, D_IN], U8, name="x_scales", align_bytes=64)
+        g_codes = mx_pool.tile([P, PASSES, D_OUT], U32, name="g_codes", align_bytes=64)
+        g_scales = mx_pool.tile([P, PASSES, D_OUT], U8, name="g_scales", align_bytes=64)
+
+        def load_partitions(raw, first, stop, pos_first):
+            rows = pos[pos_first : pos_first + PACK * (stop - first), :]
+            nc.sync.dma_start(out=raw[first:stop], in_=rows.rearrange("(p j) w -> p j w", j=PACK))
+
+        def load_last_partition(raw, first, stop, pos_first):
+            rows = pos[pos_first : pos_first + stop - first, :]
+            nc.sync.dma_start(out=raw[P - 1 : P, first:stop, :], in_=rows.rearrange("(o j) w -> o j w", o=1))
+
+        def load_x(c):
+            before_last_block = P - BLOCK_PARTITIONS
+            if c == 0:
+                load_partitions(raw_x[0], 0, before_last_block, 2)
+                load_partitions(raw_x[0], before_last_block, P - 1, 2 + PACK * before_last_block)
+                load_last_partition(raw_x[0], 0, 2, 510)
+                load_last_partition(raw_x[0], 3, 4, 512)
+            elif c == 1:
+                load_partitions(raw_x[1], 0, before_last_block, 513)
+                load_partitions(raw_x[1], before_last_block, P - 1, 513 + PACK * before_last_block)
+                load_last_partition(raw_x[1], 0, 3, 1021)
+            else:
+                load_partitions(raw_x[2], 0, P, 1024)
+
+        def load_g(c, r):
+            rows = grad[c * K_PASS : (c + 1) * K_PASS, r * ROUND_ROWS : (r + 1) * ROUND_ROWS]
+            nc.sync.dma_start(out=raw_g[c][r][:], in_=rows.rearrange("(p j) w -> p j w", j=PACK))
+
+        nc.vector.memset(raw_x[0][:, 2, :], 0.0)
+        nc.vector.memset(raw_x[1][:, 3, :], 0.0)
+
+        for c in PASS_ORDER:
+            load_g(c, 0)
+            load_x(c)
+        for c in PASS_ORDER:
+            load_g(c, 1)
+
+        def g_unit(c, r):
+            cols = slice(r * ROUND_ROWS, (r + 1) * ROUND_ROWS)
+            return (raw_g[c][r][:], g_codes[:, c, cols], g_scales[:, c, cols], E5M2_X4)
+
+        def x_unit(c, n):
+            cols = slice(n * UNIT, (n + 1) * UNIT)
+            return (raw_x[c][:, :, cols], x_codes[:, c, cols], x_scales[:, c, cols], E4M3_X4)
+
+        units = []
+        for c in PASS_ORDER:
+            units.append(g_unit(c, 0))
+            units.extend([x_unit(c, n) for n in range(D_IN // UNIT)])
+        for c in PASS_ORDER:
+            units.append(g_unit(c, 1))
+        grouped_tiles = []
+
+        def regroup(u):
+            raw = units[u][0]
+            grouped = grouped_pool.tile([P, UNIT, PACK], BF16, name="grouped", align_bytes=64)
+            grouped_tiles.append(grouped)
+            vector_cols = slice(0, VECTOR_COLS)
+            scalar_cols = slice(VECTOR_COLS, UNIT)
+            nc.vector.tensor_copy(
+                out=grouped[:, vector_cols, :].rearrange("p (c i) j -> p c j i", i=RUN),
+                in_=raw[:, :, vector_cols].rearrange("p j (c i) -> p c j i", i=RUN),
+            )
+            nc.scalar.copy(
+                out=grouped[:, scalar_cols, :].rearrange("p (c i) j -> p c j i", i=RUN),
+                in_=raw[:, :, scalar_cols].rearrange("p j (c i) -> p c j i", i=RUN),
+            )
+
+        def quantise(u):
+            codes, scales, packed_dtype = units[u][1:]
+            nc.vector.quantize_mx(
+                out=codes.bitcast(packed_dtype),
+                scales=scales,
+                in_=grouped_tiles[u][:].rearrange("p w j -> p (w j)"),
+            )
+
+        def prepare(first, stop):
+            for u in range(first, stop):
+                regroup(u)
+                if u > 0:
+                    quantise(u - 1)
+
+        def multiply(r):
+            banks = {}
+            for m in range(M_TILES):
+                for n in range(N_TILES):
+                    banks[(m, n)] = psum_pool.tile([M_TILE, N_TILE], F32, name="bank")
+            for step, c in enumerate(PASS_ORDER):
+                for m in range(M_TILES):
+                    g_cols = slice(r * ROUND_ROWS + m * M_TILE, r * ROUND_ROWS + (m + 1) * M_TILE)
+                    for n in range(N_TILES):
+                        x_cols = slice(n * N_TILE, (n + 1) * N_TILE)
+                        nc.tensor.matmul_mx(
+                            out=banks[(m, n)][:],
+                            lhsT=g_codes[:, c, g_cols].bitcast(E5M2_X4),
+                            lhsT_scale=g_scales[:, c, g_cols],
+                            rhs=x_codes[:, c, x_cols].bitcast(E4M3_X4),
+                            rhs_scale=x_scales[:, c, x_cols],
+                            start=(step == 0),
+                            stop=(step == PASSES - 1),
+                        )
+            return banks
+
+        def empty(r, banks):
+            for m in range(M_TILES):
+                out_rows = slice(r * ROUND_ROWS + m * M_TILE, r * ROUND_ROWS + (m + 1) * M_TILE)
+                for n in range(N_TILES):
+                    result = result_pool.tile([M_TILE, N_TILE], F32, name="result")
+                    if n % 2 == 0:
+                        nc.scalar.copy(out=result[:], in_=banks[(m, n)][:])
+                    else:
+                        nc.vector.tensor_copy(out=result[:], in_=banks[(m, n)][:])
+                    nc.sync.dma_start(out=out[out_rows, n * N_TILE : (n + 1) * N_TILE], in_=result[:])
+
+        round0_units = PASSES * (1 + D_IN // UNIT)
+        prepare(0, round0_units + 2)
+        banks = multiply(0)
+        empty(0, banks)
+        prepare(round0_units + 2, len(units))
+        quantise(len(units) - 1)
+        banks = multiply(1)
+        empty(1, banks)

@@ -48,6 +48,7 @@ def tile_relativemultiheadattention_pa_kernel(tc, pos_embed, W_r, b_r, grad_out,
         mx_pool = stack.enter_context(tc.tile_pool(name="mx", bufs=1))
         result_pool = stack.enter_context(tc.tile_pool(name="result", bufs=ROUNDS * M_TILES * N_TILES))
         psum_pool = stack.enter_context(tc.psum_pool(name="psum", bufs=M_TILES * N_TILES))
+        stack.enter_context(tc.manual_schedule())
 
         raw_x = [raw_pool.tile([P, PACK, D_IN], BF16, name="raw_x%d" % c) for c in range(PASSES)]
         raw_g = [
@@ -139,43 +140,53 @@ def tile_relativemultiheadattention_pa_kernel(tc, pos_embed, W_r, b_r, grad_out,
                 if u > 0:
                     quantise(u - 1)
 
-        def multiply(r):
-            banks = {}
-            for m in range(M_TILES):
-                for n in range(N_TILES):
-                    banks[(m, n)] = psum_pool.tile([M_TILE, N_TILE], F32, name="bank")
-            for step, c in enumerate(PASS_ORDER):
-                for m in range(M_TILES):
-                    g_cols = slice(r * ROUND_ROWS + m * M_TILE, r * ROUND_ROWS + (m + 1) * M_TILE)
-                    for n in range(N_TILES):
-                        x_cols = slice(n * N_TILE, (n + 1) * N_TILE)
-                        nc.tensor.matmul_mx(
-                            out=banks[(m, n)][:],
-                            lhsT=g_codes[:, c, g_cols].bitcast(E5M2_X4),
-                            lhsT_scale=g_scales[:, c, g_cols],
-                            rhs=x_codes[:, c, x_cols].bitcast(E4M3_X4),
-                            rhs_scale=x_scales[:, c, x_cols],
-                            start=(step == 0),
-                            stop=(step == PASSES - 1),
-                        )
-            return banks
+        pieces = [(m, n) for n in range(N_TILES) for m in range(M_TILES)]
+
+        def open_banks():
+            return dict([(piece, psum_pool.tile([M_TILE, N_TILE], F32, name="bank")) for piece in pieces])
+
+        def one_pass(r, banks, piece, step):
+            m, n = piece
+            c = PASS_ORDER[step]
+            g_cols = slice(r * ROUND_ROWS + m * M_TILE, r * ROUND_ROWS + (m + 1) * M_TILE)
+            x_cols = slice(n * N_TILE, (n + 1) * N_TILE)
+            nc.tensor.matmul_mx(
+                out=banks[piece][:],
+                lhsT=g_codes[:, c, g_cols].bitcast(E5M2_X4),
+                lhsT_scale=g_scales[:, c, g_cols],
+                rhs=x_codes[:, c, x_cols].bitcast(E4M3_X4),
+                rhs_scale=x_scales[:, c, x_cols],
+                start=(step == 0),
+                stop=(step == PASSES - 1),
+            )
 
         def empty(r, banks):
-            for m in range(M_TILES):
+            for turn, piece in enumerate(pieces):
+                m, n = piece
                 out_rows = slice(r * ROUND_ROWS + m * M_TILE, r * ROUND_ROWS + (m + 1) * M_TILE)
-                for n in range(N_TILES):
-                    result = result_pool.tile([M_TILE, N_TILE], F32, name="result")
-                    if n % 2 == 0:
-                        nc.scalar.copy(out=result[:], in_=banks[(m, n)][:])
-                    else:
-                        nc.vector.tensor_copy(out=result[:], in_=banks[(m, n)][:])
-                    nc.sync.dma_start(out=out[out_rows, n * N_TILE : (n + 1) * N_TILE], in_=result[:])
+                result = result_pool.tile([M_TILE, N_TILE], F32, name="result")
+                if turn % 2 == 0:
+                    nc.scalar.copy(out=result[:], in_=banks[piece][:])
+                else:
+                    nc.vector.tensor_copy(out=result[:], in_=banks[piece][:])
+                nc.sync.dma_start(out=out[out_rows, n * N_TILE : (n + 1) * N_TILE], in_=result[:])
 
         round0_units = PASSES * (1 + D_IN // UNIT)
         prepare(0, round0_units + 2)
-        banks = multiply(0)
+
+        banks = open_banks()
+        for step in range(PASSES):
+            for piece in pieces:
+                one_pass(0, banks, piece, step)
         empty(0, banks)
+
         prepare(round0_units + 2, len(units))
         quantise(len(units) - 1)
-        banks = multiply(1)
+
+        banks = open_banks()
+        for piece in pieces:
+            one_pass(1, banks, piece, 0)
+        for piece in pieces:
+            for step in range(1, PASSES):
+                one_pass(1, banks, piece, step)
         empty(1, banks)

@@ -51,10 +51,7 @@ def tile_relativemultiheadattention_pa_kernel(tc, pos_embed, W_r, b_r, grad_out,
         stack.enter_context(tc.manual_schedule())
 
         raw_x = [raw_pool.tile([P, PACK, D_IN], BF16, name="raw_x%d" % c) for c in range(PASSES)]
-        raw_g = [
-            [raw_pool.tile([P, PACK, ROUND_ROWS], BF16, name="raw_g%d_%d" % (c, r)) for r in range(ROUNDS)]
-            for c in range(PASSES)
-        ]
+        raw_g = [raw_pool.tile([P, PACK, D_OUT], BF16, name="raw_g%d" % c) for c in range(PASSES)]
         x_codes = mx_pool.tile([P, PASSES, D_IN], U32, name="x_codes", align_bytes=64)
         x_scales = mx_pool.tile([P, PASSES, D_IN], U8, name="x_scales", align_bytes=64)
         g_codes = mx_pool.tile([P, PASSES, D_OUT], U32, name="g_codes", align_bytes=64)
@@ -82,33 +79,29 @@ def tile_relativemultiheadattention_pa_kernel(tc, pos_embed, W_r, b_r, grad_out,
             else:
                 load_partitions(raw_x[2], 0, P, 1024)
 
-        def load_g(c, r):
-            rows = grad[c * K_PASS : (c + 1) * K_PASS, r * ROUND_ROWS : (r + 1) * ROUND_ROWS]
-            nc.sync.dma_start(out=raw_g[c][r][:], in_=rows.rearrange("(p j) w -> p j w", j=PACK))
+        def load_g(c):
+            rows = grad[c * K_PASS : (c + 1) * K_PASS, :]
+            nc.sync.dma_start(out=raw_g[c][:], in_=rows.rearrange("(p j) w -> p j w", j=PACK))
 
         nc.vector.memset(raw_x[0][:, 2, :], 0.0)
         nc.vector.memset(raw_x[1][:, 3, :], 0.0)
 
         for c in PASS_ORDER:
-            load_g(c, 0)
+            load_g(c)
             load_x(c)
-        for c in PASS_ORDER:
-            load_g(c, 1)
 
-        def g_unit(c, r):
-            cols = slice(r * ROUND_ROWS, (r + 1) * ROUND_ROWS)
-            return (raw_g[c][r][:], g_codes[:, c, cols], g_scales[:, c, cols], E5M2_X4)
+        def g_unit(c, i):
+            cols = slice(i * UNIT, (i + 1) * UNIT)
+            return (raw_g[c][:, :, cols], g_codes[:, c, cols], g_scales[:, c, cols], E5M2_X4)
 
-        def x_unit(c, n):
-            cols = slice(n * UNIT, (n + 1) * UNIT)
+        def x_unit(c, i):
+            cols = slice(i * UNIT, (i + 1) * UNIT)
             return (raw_x[c][:, :, cols], x_codes[:, c, cols], x_scales[:, c, cols], E4M3_X4)
 
         units = []
         for c in PASS_ORDER:
-            units.append(g_unit(c, 0))
-            units.extend([x_unit(c, n) for n in range(D_IN // UNIT)])
-        for c in PASS_ORDER:
-            units.append(g_unit(c, 1))
+            units.extend([g_unit(c, i) for i in range(D_OUT // UNIT)])
+            units.extend([x_unit(c, i) for i in range(D_IN // UNIT)])
         grouped_tiles = []
 
         def regroup(u):
@@ -171,8 +164,8 @@ def tile_relativemultiheadattention_pa_kernel(tc, pos_embed, W_r, b_r, grad_out,
                     nc.vector.tensor_copy(out=result[:], in_=banks[piece][:])
                 nc.sync.dma_start(out=out[out_rows, n * N_TILE : (n + 1) * N_TILE], in_=result[:])
 
-        round0_units = PASSES * (1 + D_IN // UNIT)
-        prepare(0, round0_units + 2)
+        prepare(0, len(units))
+        quantise(len(units) - 1)
 
         banks = open_banks()
         for step in range(PASSES):
@@ -180,13 +173,8 @@ def tile_relativemultiheadattention_pa_kernel(tc, pos_embed, W_r, b_r, grad_out,
                 one_pass(0, banks, piece, step)
         empty(0, banks)
 
-        prepare(round0_units + 2, len(units))
-        quantise(len(units) - 1)
-
         banks = open_banks()
         for piece in pieces:
-            one_pass(1, banks, piece, 0)
-        for piece in pieces:
-            for step in range(1, PASSES):
+            for step in range(PASSES):
                 one_pass(1, banks, piece, step)
         empty(1, banks)

@@ -1,6 +1,7 @@
 from contextlib import ExitStack
 
 import concourse.mybir as mybir
+from concourse.masks import make_identity
 
 BF16 = mybir.dt.bfloat16
 F32 = mybir.dt.float32
@@ -12,7 +13,6 @@ E5M2_X4 = mybir.dt.float8_e5m2_x4
 P = 128
 PACK = 4
 K_PASS = P * PACK
-BLOCK_PARTITIONS = 8
 
 TOKENS = 1536
 D_OUT = 1024
@@ -51,57 +51,75 @@ def tile_relativemultiheadattention_pa_kernel(tc, pos_embed, W_r, b_r, grad_out,
         stack.enter_context(tc.manual_schedule())
 
         raw_x = [raw_pool.tile([P, PACK, D_IN], BF16, name="raw_x%d" % c) for c in range(PASSES)]
-        raw_g = [raw_pool.tile([P, PACK, D_OUT], BF16, name="raw_g%d" % c) for c in range(PASSES)]
+        raw_g = [
+            [raw_pool.tile([P, PACK, ROUND_ROWS], BF16, name="raw_g%d_%d" % (c, r)) for r in range(ROUNDS)]
+            for c in range(PASSES)
+        ]
         x_codes = mx_pool.tile([P, PASSES, D_IN], U32, name="x_codes", align_bytes=64)
         x_scales = mx_pool.tile([P, PASSES, D_IN], U8, name="x_scales", align_bytes=64)
         g_codes = mx_pool.tile([P, PASSES, D_OUT], U32, name="g_codes", align_bytes=64)
         g_scales = mx_pool.tile([P, PASSES, D_OUT], U8, name="g_scales", align_bytes=64)
 
-        def load_partitions(raw, first, stop, pos_first):
-            rows = pos[pos_first : pos_first + PACK * (stop - first), :]
-            nc.sync.dma_start(out=raw[first:stop], in_=rows.rearrange("(p j) w -> p j w", j=PACK))
-
-        def load_last_partition(raw, first, stop, pos_first):
-            rows = pos[pos_first : pos_first + stop - first, :]
-            nc.sync.dma_start(out=raw[P - 1 : P, first:stop, :], in_=rows.rearrange("(o j) w -> o j w", o=1))
+        identity = raw_pool.tile([P, P], F32, name="identity")
+        make_identity(nc, identity[:])
+        keep = raw_pool.tile([P, 1], F32, name="keep")
+        nc.vector.tensor_scalar(
+            out=keep[:],
+            in0=identity[:, P - 1 : P],
+            scalar1=-1.0,
+            scalar2=1.0,
+            op0=mybir.AluOpType.mult,
+            op1=mybir.AluOpType.add,
+        )
+        row_511 = raw_pool.tile([P, D_IN], BF16, name="row_511")
+        nc.vector.memset(row_511[:], 0.0)
+        nc.scalar.dma_start(out=row_511[P - 1 : P, :], in_=pos[512:513, :])
 
         def load_x(c):
-            before_last_block = P - BLOCK_PARTITIONS
+            pos_first = (2, 513, 1024)[c]
+            rows = pos[pos_first : pos_first + K_PASS, :]
+            nc.sync.dma_start(out=raw_x[c][:], in_=rows.rearrange("(p j) w -> p j w", j=PACK))
+
+        def mend_x(c):
             if c == 0:
-                load_partitions(raw_x[0], 0, before_last_block, 2)
-                load_partitions(raw_x[0], before_last_block, P - 1, 2 + PACK * before_last_block)
-                load_last_partition(raw_x[0], 0, 2, 510)
-                load_last_partition(raw_x[0], 3, 4, 512)
+                nc.vector.tensor_scalar_mul(out=raw_x[0][:, 2, :], in0=raw_x[0][:, 2, :], scalar1=keep[:, 0:1])
+                nc.vector.scalar_tensor_tensor(
+                    out=raw_x[0][:, 3, :],
+                    in0=raw_x[0][:, 3, :],
+                    scalar=keep[:, 0:1],
+                    in1=row_511[:],
+                    op0=mybir.AluOpType.mult,
+                    op1=mybir.AluOpType.add,
+                )
             elif c == 1:
-                load_partitions(raw_x[1], 0, before_last_block, 513)
-                load_partitions(raw_x[1], before_last_block, P - 1, 513 + PACK * before_last_block)
-                load_last_partition(raw_x[1], 0, 3, 1021)
-            else:
-                load_partitions(raw_x[2], 0, P, 1024)
+                nc.vector.tensor_scalar_mul(out=raw_x[1][:, 3, :], in0=raw_x[1][:, 3, :], scalar1=keep[:, 0:1])
 
-        def load_g(c):
-            rows = grad[c * K_PASS : (c + 1) * K_PASS, :]
-            nc.sync.dma_start(out=raw_g[c][:], in_=rows.rearrange("(p j) w -> p j w", j=PACK))
-
-        nc.vector.memset(raw_x[0][:, 2, :], 0.0)
-        nc.vector.memset(raw_x[1][:, 3, :], 0.0)
+        def load_g(c, r):
+            rows = grad[c * K_PASS : (c + 1) * K_PASS, r * ROUND_ROWS : (r + 1) * ROUND_ROWS]
+            nc.sync.dma_start(out=raw_g[c][r][:], in_=rows.rearrange("(p j) w -> p j w", j=PACK))
 
         for c in PASS_ORDER:
-            load_g(c)
+            load_g(c, 0)
             load_x(c)
+        for c in PASS_ORDER:
+            load_g(c, 1)
 
-        def g_unit(c, i):
-            cols = slice(i * UNIT, (i + 1) * UNIT)
-            return (raw_g[c][:, :, cols], g_codes[:, c, cols], g_scales[:, c, cols], E5M2_X4)
+        def g_unit(c, r):
+            cols = slice(r * ROUND_ROWS, (r + 1) * ROUND_ROWS)
+            return (raw_g[c][r][:], g_codes[:, c, cols], g_scales[:, c, cols], E5M2_X4)
 
-        def x_unit(c, i):
-            cols = slice(i * UNIT, (i + 1) * UNIT)
+        def x_unit(c, n):
+            cols = slice(n * UNIT, (n + 1) * UNIT)
             return (raw_x[c][:, :, cols], x_codes[:, c, cols], x_scales[:, c, cols], E4M3_X4)
 
         units = []
+        mend_before = {}
         for c in PASS_ORDER:
-            units.extend([g_unit(c, i) for i in range(D_OUT // UNIT)])
-            units.extend([x_unit(c, i) for i in range(D_IN // UNIT)])
+            units.append(g_unit(c, 0))
+            mend_before[len(units)] = c
+            units.extend([x_unit(c, n) for n in range(D_IN // UNIT)])
+        for c in PASS_ORDER:
+            units.append(g_unit(c, 1))
         grouped_tiles = []
 
         def regroup(u):
@@ -129,6 +147,8 @@ def tile_relativemultiheadattention_pa_kernel(tc, pos_embed, W_r, b_r, grad_out,
 
         def prepare(first, stop):
             for u in range(first, stop):
+                if u in mend_before:
+                    mend_x(mend_before[u])
                 regroup(u)
                 if u > 0:
                     quantise(u - 1)
@@ -164,8 +184,8 @@ def tile_relativemultiheadattention_pa_kernel(tc, pos_embed, W_r, b_r, grad_out,
                     nc.vector.tensor_copy(out=result[:], in_=banks[piece][:])
                 nc.sync.dma_start(out=out[out_rows, n * N_TILE : (n + 1) * N_TILE], in_=result[:])
 
-        prepare(0, len(units))
-        quantise(len(units) - 1)
+        round0_units = PASSES * (1 + D_IN // UNIT)
+        prepare(0, round0_units + 2)
 
         banks = open_banks()
         for step in range(PASSES):
@@ -173,8 +193,13 @@ def tile_relativemultiheadattention_pa_kernel(tc, pos_embed, W_r, b_r, grad_out,
                 one_pass(0, banks, piece, step)
         empty(0, banks)
 
+        prepare(round0_units + 2, len(units))
+        quantise(len(units) - 1)
+
         banks = open_banks()
         for piece in pieces:
-            for step in range(PASSES):
+            one_pass(1, banks, piece, 0)
+        for piece in pieces:
+            for step in range(1, PASSES):
                 one_pass(1, banks, piece, step)
         empty(1, banks)

@@ -9,6 +9,8 @@ U32 = mybir.dt.uint32
 U8 = mybir.dt.uint8
 E4M3_X4 = mybir.dt.float8_e4m3fn_x4
 E5M2_X4 = mybir.dt.float8_e5m2_x4
+MULT = mybir.AluOpType.mult
+ADD = mybir.AluOpType.add
 
 P = 128
 PACK = 4
@@ -31,6 +33,7 @@ RUN = 4
 VECTOR_COLS = UNIT // 2
 GROUPED_BUFS = 4
 
+X_PASS_STARTS_AT_POS = (2, 513, 1024)
 PASS_ORDER = (2, 1, 0)
 
 FLOPS = 2 * TOKENS * D_OUT * D_IN
@@ -42,7 +45,15 @@ def tile_relativemultiheadattention_pa_kernel(tc, pos_embed, W_r, b_r, grad_out,
     pos = pos_embed.flatten_outer_dims()
     grad = grad_out.flatten_outer_dims()
 
+    units = []
+    for c in PASS_ORDER:
+        units.append(("g", c, 0))
+        units.extend([("x", c, n) for n in range(N_TILES)])
+    round0_units = len(units)
+    units.extend([("g", c, 1) for c in PASS_ORDER])
+
     with ExitStack() as stack:
+        const_pool = stack.enter_context(tc.tile_pool(name="const", bufs=1))
         raw_pool = stack.enter_context(tc.tile_pool(name="raw", bufs=1))
         grouped_pool = stack.enter_context(tc.tile_pool(name="grouped", bufs=GROUPED_BUFS))
         mx_pool = stack.enter_context(tc.tile_pool(name="mx", bufs=1))
@@ -50,53 +61,38 @@ def tile_relativemultiheadattention_pa_kernel(tc, pos_embed, W_r, b_r, grad_out,
         psum_pool = stack.enter_context(tc.psum_pool(name="psum", bufs=M_TILES * N_TILES))
         stack.enter_context(tc.manual_schedule())
 
-        raw_x = [raw_pool.tile([P, PACK, D_IN], BF16, name="raw_x%d" % c) for c in range(PASSES)]
         raw_g = [
             [raw_pool.tile([P, PACK, ROUND_ROWS], BF16, name="raw_g%d_%d" % (c, r)) for r in range(ROUNDS)]
             for c in range(PASSES)
         ]
-        x_codes = mx_pool.tile([P, PASSES, D_IN], U32, name="x_codes", align_bytes=64)
-        x_scales = mx_pool.tile([P, PASSES, D_IN], U8, name="x_scales", align_bytes=64)
-        g_codes = mx_pool.tile([P, PASSES, D_OUT], U32, name="g_codes", align_bytes=64)
-        g_scales = mx_pool.tile([P, PASSES, D_OUT], U8, name="g_scales", align_bytes=64)
+        raw_x = [raw_pool.tile([P, PACK, D_IN], BF16, name="raw_x%d" % c) for c in range(PASSES)]
+        codes = {
+            "g": mx_pool.tile([P, PASSES, D_OUT], U32, name="g_codes", align_bytes=64),
+            "x": mx_pool.tile([P, PASSES, D_IN], U32, name="x_codes", align_bytes=64),
+        }
+        scales = {
+            "g": mx_pool.tile([P, PASSES, D_OUT], U8, name="g_scales", align_bytes=64),
+            "x": mx_pool.tile([P, PASSES, D_IN], U8, name="x_scales", align_bytes=64),
+        }
+        packed_dtype = {"g": E5M2_X4, "x": E4M3_X4}
 
-        identity = raw_pool.tile([P, P], F32, name="identity")
+        identity = const_pool.tile([P, P], F32, name="identity")
         make_identity(nc, identity[:])
-        keep = raw_pool.tile([P, 1], F32, name="keep")
+        keep = const_pool.tile([P, 1], F32, name="keep")
         nc.vector.tensor_scalar(
-            out=keep[:],
-            in0=identity[:, P - 1 : P],
-            scalar1=-1.0,
-            scalar2=1.0,
-            op0=mybir.AluOpType.mult,
-            op1=mybir.AluOpType.add,
+            out=keep[:], in0=identity[:, P - 1 : P], scalar1=-1.0, scalar2=1.0, op0=MULT, op1=ADD
         )
-        row_511 = raw_pool.tile([P, D_IN], BF16, name="row_511")
-        nc.vector.memset(row_511[:], 0.0)
-        nc.scalar.dma_start(out=row_511[P - 1 : P, :], in_=pos[512:513, :])
-
-        def load_x(c):
-            pos_first = (2, 513, 1024)[c]
-            rows = pos[pos_first : pos_first + K_PASS, :]
-            nc.sync.dma_start(out=raw_x[c][:], in_=rows.rearrange("(p j) w -> p j w", j=PACK))
-
-        def mend_x(c):
-            if c == 0:
-                nc.vector.tensor_scalar_mul(out=raw_x[0][:, 2, :], in0=raw_x[0][:, 2, :], scalar1=keep[:, 0:1])
-                nc.vector.scalar_tensor_tensor(
-                    out=raw_x[0][:, 3, :],
-                    in0=raw_x[0][:, 3, :],
-                    scalar=keep[:, 0:1],
-                    in1=row_511[:],
-                    op0=mybir.AluOpType.mult,
-                    op1=mybir.AluOpType.add,
-                )
-            elif c == 1:
-                nc.vector.tensor_scalar_mul(out=raw_x[1][:, 3, :], in0=raw_x[1][:, 3, :], scalar1=keep[:, 0:1])
+        x_row_511 = const_pool.tile([P, D_IN], BF16, name="x_row_511")
+        nc.vector.memset(x_row_511[:], 0.0)
+        nc.scalar.dma_start(out=x_row_511[P - 1 : P, :], in_=pos[512:513, :])
 
         def load_g(c, r):
             rows = grad[c * K_PASS : (c + 1) * K_PASS, r * ROUND_ROWS : (r + 1) * ROUND_ROWS]
             nc.sync.dma_start(out=raw_g[c][r][:], in_=rows.rearrange("(p j) w -> p j w", j=PACK))
+
+        def load_x(c):
+            rows = pos[X_PASS_STARTS_AT_POS[c] : X_PASS_STARTS_AT_POS[c] + K_PASS, :]
+            nc.sync.dma_start(out=raw_x[c][:], in_=rows.rearrange("(p j) w -> p j w", j=PACK))
 
         for c in PASS_ORDER:
             load_g(c, 0)
@@ -104,26 +100,23 @@ def tile_relativemultiheadattention_pa_kernel(tc, pos_embed, W_r, b_r, grad_out,
         for c in PASS_ORDER:
             load_g(c, 1)
 
-        def g_unit(c, r):
-            cols = slice(r * ROUND_ROWS, (r + 1) * ROUND_ROWS)
-            return (raw_g[c][r][:], g_codes[:, c, cols], g_scales[:, c, cols], E5M2_X4)
+        def mend_x(c):
+            if c == 0:
+                last_slots = raw_x[0][:, 2:4, :]
+                nc.vector.tensor_scalar_mul(out=last_slots, in0=last_slots, scalar1=keep[:, 0:1])
+                nc.vector.tensor_tensor(out=raw_x[0][:, 3, :], in0=raw_x[0][:, 3, :], in1=x_row_511[:], op=ADD)
+            if c == 1:
+                last_slot = raw_x[1][:, 3, :]
+                nc.vector.tensor_scalar_mul(out=last_slot, in0=last_slot, scalar1=keep[:, 0:1])
 
-        def x_unit(c, n):
-            cols = slice(n * UNIT, (n + 1) * UNIT)
-            return (raw_x[c][:, :, cols], x_codes[:, c, cols], x_scales[:, c, cols], E4M3_X4)
-
-        units = []
-        mend_before = {}
-        for c in PASS_ORDER:
-            units.append(g_unit(c, 0))
-            mend_before[len(units)] = c
-            units.extend([x_unit(c, n) for n in range(D_IN // UNIT)])
-        for c in PASS_ORDER:
-            units.append(g_unit(c, 1))
         grouped_tiles = []
 
         def regroup(u):
-            raw = units[u][0]
+            operand, c, block = units[u]
+            if operand == "g":
+                raw = raw_g[c][block][:]
+            else:
+                raw = raw_x[c][:, :, block * UNIT : (block + 1) * UNIT]
             grouped = grouped_pool.tile([P, UNIT, PACK], BF16, name="grouped", align_bytes=64)
             grouped_tiles.append(grouped)
             vector_cols = slice(0, VECTOR_COLS)
@@ -138,17 +131,19 @@ def tile_relativemultiheadattention_pa_kernel(tc, pos_embed, W_r, b_r, grad_out,
             )
 
         def quantise(u):
-            codes, scales, packed_dtype = units[u][1:]
+            operand, c, block = units[u]
+            cols = slice(block * UNIT, (block + 1) * UNIT)
             nc.vector.quantize_mx(
-                out=codes.bitcast(packed_dtype),
-                scales=scales,
+                out=codes[operand][:, c, cols].bitcast(packed_dtype[operand]),
+                scales=scales[operand][:, c, cols],
                 in_=grouped_tiles[u][:].rearrange("p w j -> p (w j)"),
             )
 
         def prepare(first, stop):
             for u in range(first, stop):
-                if u in mend_before:
-                    mend_x(mend_before[u])
+                operand, c, block = units[u]
+                if operand == "x" and block == 0:
+                    mend_x(c)
                 regroup(u)
                 if u > 0:
                     quantise(u - 1)
@@ -165,10 +160,10 @@ def tile_relativemultiheadattention_pa_kernel(tc, pos_embed, W_r, b_r, grad_out,
             x_cols = slice(n * N_TILE, (n + 1) * N_TILE)
             nc.tensor.matmul_mx(
                 out=banks[piece][:],
-                lhsT=g_codes[:, c, g_cols].bitcast(E5M2_X4),
-                lhsT_scale=g_scales[:, c, g_cols],
-                rhs=x_codes[:, c, x_cols].bitcast(E4M3_X4),
-                rhs_scale=x_scales[:, c, x_cols],
+                lhsT=codes["g"][:, c, g_cols].bitcast(E5M2_X4),
+                lhsT_scale=scales["g"][:, c, g_cols],
+                rhs=codes["x"][:, c, x_cols].bitcast(E4M3_X4),
+                rhs_scale=scales["x"][:, c, x_cols],
                 start=(step == 0),
                 stop=(step == PASSES - 1),
             )
@@ -184,7 +179,6 @@ def tile_relativemultiheadattention_pa_kernel(tc, pos_embed, W_r, b_r, grad_out,
                     nc.vector.tensor_copy(out=result[:], in_=banks[piece][:])
                 nc.sync.dma_start(out=out[out_rows, n * N_TILE : (n + 1) * N_TILE], in_=result[:])
 
-        round0_units = PASSES * (1 + D_IN // UNIT)
         prepare(0, round0_units + 2)
 
         banks = open_banks()

@@ -23,15 +23,15 @@ PASSES = TOKENS // K_PASS
 
 M_TILE = 128
 N_TILE = 512
-ROUNDS = 2
-ROUND_ROWS = D_OUT // ROUNDS
-M_TILES = ROUND_ROWS // M_TILE
+BANKS = 8
 N_TILES = D_IN // N_TILE
 
-UNIT = 512
+LOAD_COLS = 512
 RUN = 4
-VECTOR_COLS = UNIT // 2
 GROUPED_BUFS = 4
+
+V_COLS_PLAIN = 240
+V_COLS_X = {2: 240, 1: 208, 0: 176}
 
 X_PASS_STARTS_AT_POS = (2, 513, 1024)
 PASS_ORDER = (2, 1, 0)
@@ -47,25 +47,30 @@ def tile_relativemultiheadattention_pa_kernel(tc, pos_embed, W_r, b_r, grad_out,
 
     units = []
     for c in PASS_ORDER:
-        units.append(("g", c, 0))
-        units.extend([("x", c, n) for n in range(N_TILES)])
-    round0_units = len(units)
-    units.extend([("g", c, 1) for c in PASS_ORDER])
+        units.append(("g", c, 0, 512, V_COLS_PLAIN))
+        units.append(("x", c, 0, 512, V_COLS_X[c]))
+        units.append(("x", c, 512, 512, V_COLS_X[c]))
+    first_part = len(units)
+    for col0 in (512, 768):
+        for c in PASS_ORDER:
+            units.append(("g", c, col0, 256, 256))
 
     with ExitStack() as stack:
         const_pool = stack.enter_context(tc.tile_pool(name="const", bufs=1))
         raw_pool = stack.enter_context(tc.tile_pool(name="raw", bufs=1))
         grouped_pool = stack.enter_context(tc.tile_pool(name="grouped", bufs=GROUPED_BUFS))
         mx_pool = stack.enter_context(tc.tile_pool(name="mx", bufs=1))
-        result_pool = stack.enter_context(tc.tile_pool(name="result", bufs=ROUNDS * M_TILES * N_TILES))
-        psum_pool = stack.enter_context(tc.psum_pool(name="psum", bufs=M_TILES * N_TILES))
+        result_pool = stack.enter_context(tc.tile_pool(name="result", bufs=2 * BANKS))
+        psum_pool = stack.enter_context(tc.psum_pool(name="psum", bufs=BANKS))
         stack.enter_context(tc.manual_schedule())
 
-        raw_g = [
-            [raw_pool.tile([P, PACK, ROUND_ROWS], BF16, name="raw_g%d_%d" % (c, r)) for r in range(ROUNDS)]
-            for c in range(PASSES)
-        ]
-        raw_x = [raw_pool.tile([P, PACK, D_IN], BF16, name="raw_x%d" % c) for c in range(PASSES)]
+        raw = {}
+        for operand in ("g", "x"):
+            for c in range(PASSES):
+                for half in range(2):
+                    raw[(operand, c, half)] = raw_pool.tile(
+                        [P, PACK, LOAD_COLS], BF16, name="raw_%s%d_%d" % (operand, c, half)
+                    )
         codes = {
             "g": mx_pool.tile([P, PASSES, D_OUT], U32, name="g_codes", align_bytes=64),
             "x": mx_pool.tile([P, PASSES, D_IN], U32, name="x_codes", align_bytes=64),
@@ -86,114 +91,125 @@ def tile_relativemultiheadattention_pa_kernel(tc, pos_embed, W_r, b_r, grad_out,
         nc.vector.memset(x_row_511[:], 0.0)
         nc.scalar.dma_start(out=x_row_511[P - 1 : P, :], in_=pos[512:513, :])
 
-        def load_g(c, r):
-            rows = grad[c * K_PASS : (c + 1) * K_PASS, r * ROUND_ROWS : (r + 1) * ROUND_ROWS]
-            nc.sync.dma_start(out=raw_g[c][r][:], in_=rows.rearrange("(p j) w -> p j w", j=PACK))
-
-        def load_x(c):
-            rows = pos[X_PASS_STARTS_AT_POS[c] : X_PASS_STARTS_AT_POS[c] + K_PASS, :]
-            nc.sync.dma_start(out=raw_x[c][:], in_=rows.rearrange("(p j) w -> p j w", j=PACK))
+        def load(operand, c, half):
+            cols = slice(half * LOAD_COLS, (half + 1) * LOAD_COLS)
+            if operand == "g":
+                rows = grad[c * K_PASS : (c + 1) * K_PASS, cols]
+            else:
+                rows = pos[X_PASS_STARTS_AT_POS[c] : X_PASS_STARTS_AT_POS[c] + K_PASS, cols]
+            nc.sync.dma_start(out=raw[(operand, c, half)][:], in_=rows.rearrange("(p j) w -> p j w", j=PACK))
 
         for c in PASS_ORDER:
-            load_g(c, 0)
-            load_x(c)
+            load("g", c, 0)
+            load("x", c, 0)
+            load("x", c, 1)
         for c in PASS_ORDER:
-            load_g(c, 1)
+            load("g", c, 1)
 
-        def mend_x(c):
+        def mend_x(c, half):
+            tile = raw[("x", c, half)]
             if c == 0:
-                last_slots = raw_x[0][:, 2:4, :]
-                nc.vector.tensor_scalar_mul(out=last_slots, in0=last_slots, scalar1=keep[:, 0:1])
-                nc.vector.tensor_tensor(out=raw_x[0][:, 3, :], in0=raw_x[0][:, 3, :], in1=x_row_511[:], op=ADD)
+                nc.vector.tensor_scalar_mul(out=tile[:, 2, :], in0=tile[:, 2, :], scalar1=keep[:, 0:1])
+                nc.vector.scalar_tensor_tensor(
+                    out=tile[:, 3, :],
+                    in0=tile[:, 3, :],
+                    scalar=keep[:, 0:1],
+                    in1=x_row_511[:, half * LOAD_COLS : (half + 1) * LOAD_COLS],
+                    op0=MULT,
+                    op1=ADD,
+                )
             if c == 1:
-                last_slot = raw_x[1][:, 3, :]
-                nc.vector.tensor_scalar_mul(out=last_slot, in0=last_slot, scalar1=keep[:, 0:1])
+                nc.vector.tensor_scalar_mul(out=tile[:, 3, :], in0=tile[:, 3, :], scalar1=keep[:, 0:1])
 
         grouped_tiles = []
 
         def regroup(u):
-            operand, c, block = units[u]
-            if operand == "g":
-                raw = raw_g[c][block][:]
-            else:
-                raw = raw_x[c][:, :, block * UNIT : (block + 1) * UNIT]
-            grouped = grouped_pool.tile([P, UNIT, PACK], BF16, name="grouped", align_bytes=64)
+            operand, c, col0, cols, v_cols = units[u]
+            first = col0 % LOAD_COLS
+            source = raw[(operand, c, col0 // LOAD_COLS)][:, :, first : first + cols]
+            grouped = grouped_pool.tile([P, cols, PACK], BF16, name="grouped", align_bytes=64)
             grouped_tiles.append(grouped)
-            vector_cols = slice(0, VECTOR_COLS)
-            scalar_cols = slice(VECTOR_COLS, UNIT)
             nc.vector.tensor_copy(
-                out=grouped[:, vector_cols, :].rearrange("p (c i) j -> p c j i", i=RUN),
-                in_=raw[:, :, vector_cols].rearrange("p j (c i) -> p c j i", i=RUN),
+                out=grouped[:, 0:v_cols, :].rearrange("p (c i) j -> p c j i", i=RUN),
+                in_=source[:, :, 0:v_cols].rearrange("p j (c i) -> p c j i", i=RUN),
             )
-            nc.scalar.copy(
-                out=grouped[:, scalar_cols, :].rearrange("p (c i) j -> p c j i", i=RUN),
-                in_=raw[:, :, scalar_cols].rearrange("p j (c i) -> p c j i", i=RUN),
-            )
+            if v_cols < cols:
+                nc.scalar.copy(
+                    out=grouped[:, v_cols:cols, :].rearrange("p (c i) j -> p c j i", i=RUN),
+                    in_=source[:, :, v_cols:cols].rearrange("p j (c i) -> p c j i", i=RUN),
+                )
 
         def quantise(u):
-            operand, c, block = units[u]
-            cols = slice(block * UNIT, (block + 1) * UNIT)
+            operand, c, col0, cols, v_cols = units[u]
             nc.vector.quantize_mx(
-                out=codes[operand][:, c, cols].bitcast(packed_dtype[operand]),
-                scales=scales[operand][:, c, cols],
+                out=codes[operand][:, c, col0 : col0 + cols].bitcast(packed_dtype[operand]),
+                scales=scales[operand][:, c, col0 : col0 + cols],
                 in_=grouped_tiles[u][:].rearrange("p w j -> p (w j)"),
             )
 
-        def prepare(first, stop):
-            for u in range(first, stop):
-                operand, c, block = units[u]
-                if operand == "x" and block == 0:
-                    mend_x(c)
-                regroup(u)
-                if u > 0:
-                    quantise(u - 1)
+        banks = {}
 
-        pieces = [(m, n) for n in range(N_TILES) for m in range(M_TILES)]
-
-        def open_banks():
-            return dict([(piece, psum_pool.tile([M_TILE, N_TILE], F32, name="bank")) for piece in pieces])
-
-        def one_pass(r, banks, piece, step):
-            m, n = piece
-            c = PASS_ORDER[step]
-            g_cols = slice(r * ROUND_ROWS + m * M_TILE, r * ROUND_ROWS + (m + 1) * M_TILE)
+        def one_pass(m, n, c):
+            if c == PASS_ORDER[0]:
+                banks[(m, n)] = psum_pool.tile([M_TILE, N_TILE], F32, name="bank")
+            g_cols = slice(m * M_TILE, (m + 1) * M_TILE)
             x_cols = slice(n * N_TILE, (n + 1) * N_TILE)
             nc.tensor.matmul_mx(
-                out=banks[piece][:],
+                out=banks[(m, n)][:],
                 lhsT=codes["g"][:, c, g_cols].bitcast(E5M2_X4),
                 lhsT_scale=scales["g"][:, c, g_cols],
                 rhs=codes["x"][:, c, x_cols].bitcast(E4M3_X4),
                 rhs_scale=scales["x"][:, c, x_cols],
-                start=(step == 0),
-                stop=(step == PASSES - 1),
+                start=(c == PASS_ORDER[0]),
+                stop=(c == PASS_ORDER[-1]),
             )
 
-        def empty(r, banks):
-            for turn, piece in enumerate(pieces):
-                m, n = piece
-                out_rows = slice(r * ROUND_ROWS + m * M_TILE, r * ROUND_ROWS + (m + 1) * M_TILE)
-                result = result_pool.tile([M_TILE, N_TILE], F32, name="result")
-                if turn % 2 == 0:
-                    nc.scalar.copy(out=result[:], in_=banks[piece][:])
-                else:
-                    nc.vector.tensor_copy(out=result[:], in_=banks[piece][:])
-                nc.sync.dma_start(out=out[out_rows, n * N_TILE : (n + 1) * N_TILE], in_=result[:])
+        def empty(m, n, engine):
+            result = result_pool.tile([M_TILE, N_TILE], F32, name="result")
+            if engine == "scalar":
+                nc.scalar.copy(out=result[:], in_=banks[(m, n)][:])
+            else:
+                nc.vector.tensor_copy(out=result[:], in_=banks[(m, n)][:])
+            nc.sync.dma_start(
+                out=out[m * M_TILE : (m + 1) * M_TILE, n * N_TILE : (n + 1) * N_TILE], in_=result[:]
+            )
 
-        prepare(0, round0_units + 2)
+        def matmuls_after(u):
+            operand, c, col0, cols, v_cols = units[u]
+            if u < first_part:
+                if operand == "x":
+                    for m in range(4):
+                        one_pass(m, col0 // N_TILE, c)
+            elif col0 == 512:
+                for n in range(N_TILES):
+                    for m in (4, 5):
+                        one_pass(m, n, c)
+            elif u == len(units) - 1:
+                for n in range(N_TILES):
+                    for m in (6, 7):
+                        for cc in PASS_ORDER:
+                            one_pass(m, n, cc)
 
-        banks = open_banks()
-        for step in range(PASSES):
-            for piece in pieces:
-                one_pass(0, banks, piece, step)
-        empty(0, banks)
-
-        prepare(round0_units + 2, len(units))
-        quantise(len(units) - 1)
-
-        banks = open_banks()
-        for piece in pieces:
-            one_pass(1, banks, piece, 0)
-        for piece in pieces:
-            for step in range(1, PASSES):
-                one_pass(1, banks, piece, step)
-        empty(1, banks)
+        for u in range(len(units) + 1):
+            if u < len(units):
+                operand, c, col0, cols, v_cols = units[u]
+                if operand == "x":
+                    mend_x(c, col0 // LOAD_COLS)
+                regroup(u)
+            if u > 0:
+                quantise(u - 1)
+                matmuls_after(u - 1)
+            if u == first_part:
+                for m in range(4):
+                    empty(m, 0, "scalar")
+            if u == first_part + 1:
+                for m in range(4):
+                    empty(m, 1, "scalar")
+        empty(4, 0, "scalar")
+        empty(4, 1, "scalar")
+        empty(5, 0, "vector")
+        empty(5, 1, "vector")
+        empty(6, 0, "scalar")
+        empty(7, 0, "vector")
+        empty(6, 1, "scalar")
+        empty(7, 1, "vector")

@@ -26,15 +26,21 @@ N_TILE = 512
 BANKS = 8
 N_TILES = D_IN // N_TILE
 
-LOAD_COLS = 512
 RUN = 4
 GROUPED_BUFS = 4
 
-V_COLS_PLAIN = 240
-V_COLS_X = {2: 240, 1: 208, 0: 176}
+V_COLS_G = 240
+V_COLS_X = {}
+EAGER = 0
 
 X_PASS_STARTS_AT_POS = (2, 513, 1024)
 PASS_ORDER = (2, 1, 0)
+
+LOAD_PLAN = "x"
+FILL = False
+
+LOADS = [("g",2,0,512),("g",1,0,512),("g",0,0,512),("x",2,0,512),("x",2,512,512),("x",1,0,512),("x",1,512,512),("x",0,0,512),("x",0,512,512),("g",2,512,512),("g",1,512,512),("g",0,512,512)]
+UNITS = [("g",2,0,512,240),("g",1,0,512,240),("g",0,0,512,240),("x",2,0,512,240),("x",2,512,512,240),("x",1,0,512,208),("x",1,512,512,208),("x",0,0,512,176),("x",0,512,512,176),("g",2,512,256,256),("g",1,512,256,256),("g",0,512,256,256),("g",2,768,256,256),("g",1,768,256,256),("g",0,768,256,256)]
 
 FLOPS = 2 * TOKENS * D_OUT * D_IN
 BYTES = 2 * (TOKENS - 2) * D_IN + 2 * TOKENS * D_OUT + 4 * D_OUT * D_IN
@@ -44,16 +50,9 @@ def tile_relativemultiheadattention_pa_kernel(tc, pos_embed, W_r, b_r, grad_out,
     nc = tc.nc
     pos = pos_embed.flatten_outer_dims()
     grad = grad_out.flatten_outer_dims()
-
-    units = []
-    for c in PASS_ORDER:
-        units.append(("g", c, 0, 512, V_COLS_PLAIN))
-        units.append(("x", c, 0, 512, V_COLS_X[c]))
-        units.append(("x", c, 512, 512, V_COLS_X[c]))
-    first_part = len(units)
-    for col0 in (512, 768):
-        for c in PASS_ORDER:
-            units.append(("g", c, col0, 256, 256))
+    loads = LOADS
+    units = UNITS
+    shared_units = len([unit for unit in units if unit[4] < unit[3]])
 
     with ExitStack() as stack:
         const_pool = stack.enter_context(tc.tile_pool(name="const", bufs=1))
@@ -64,13 +63,13 @@ def tile_relativemultiheadattention_pa_kernel(tc, pos_embed, W_r, b_r, grad_out,
         psum_pool = stack.enter_context(tc.psum_pool(name="psum", bufs=BANKS))
         stack.enter_context(tc.manual_schedule())
 
-        raw = {}
-        for operand in ("g", "x"):
-            for c in range(PASSES):
-                for half in range(2):
-                    raw[(operand, c, half)] = raw_pool.tile(
-                        [P, PACK, LOAD_COLS], BF16, name="raw_%s%d_%d" % (operand, c, half)
-                    )
+        raw_at = {}
+        raw_tiles = []
+        for operand, c, col0, cols in loads:
+            raw_tile = raw_pool.tile([P, PACK, cols], BF16, name="raw_%s%d_%d" % (operand, c, col0))
+            raw_tiles.append(raw_tile)
+            for offset in range(0, cols, 256):
+                raw_at[(operand, c, col0 + offset)] = (raw_tile, offset)
         codes = {
             "g": mx_pool.tile([P, PASSES, D_OUT], U32, name="g_codes", align_bytes=64),
             "x": mx_pool.tile([P, PASSES, D_IN], U32, name="x_codes", align_bytes=64),
@@ -89,44 +88,34 @@ def tile_relativemultiheadattention_pa_kernel(tc, pos_embed, W_r, b_r, grad_out,
         )
         x_row_511 = const_pool.tile([P, D_IN], BF16, name="x_row_511")
         nc.vector.memset(x_row_511[:], 0.0)
-        nc.scalar.dma_start(out=x_row_511[P - 1 : P, :], in_=pos[512:513, :])
 
-        def load(operand, c, half):
-            cols = slice(half * LOAD_COLS, (half + 1) * LOAD_COLS)
+        for raw_tile, (operand, c, col0, cols) in zip(raw_tiles, loads):
             if operand == "g":
-                rows = grad[c * K_PASS : (c + 1) * K_PASS, cols]
+                rows = grad[c * K_PASS : (c + 1) * K_PASS, col0 : col0 + cols]
             else:
-                rows = pos[X_PASS_STARTS_AT_POS[c] : X_PASS_STARTS_AT_POS[c] + K_PASS, cols]
-            nc.sync.dma_start(out=raw[(operand, c, half)][:], in_=rows.rearrange("(p j) w -> p j w", j=PACK))
+                rows = pos[X_PASS_STARTS_AT_POS[c] : X_PASS_STARTS_AT_POS[c] + K_PASS, col0 : col0 + cols]
+            if (operand, c) == ("x", 0):
+                nc.sync.dma_start(out=x_row_511[P - 1 : P, :], in_=pos[512:513, :])
+            nc.sync.dma_start(out=raw_tile[:], in_=rows.rearrange("(p j) w -> p j w", j=PACK))
 
-        for c in PASS_ORDER:
-            load("g", c, 0)
-            load("x", c, 0)
-            load("x", c, 1)
-        for c in PASS_ORDER:
-            load("g", c, 1)
-
-        def mend_x(c, half):
-            tile = raw[("x", c, half)]
+        def mend_x(c, col0, cols):
+            tile, offset = raw_at[("x", c, col0)]
+            span = slice(offset, offset + cols)
+            row_span = slice(col0, col0 + cols)
             if c == 0:
-                nc.vector.tensor_scalar_mul(out=tile[:, 2, :], in0=tile[:, 2, :], scalar1=keep[:, 0:1])
+                nc.vector.tensor_scalar_mul(out=tile[:, 2, span], in0=tile[:, 2, span], scalar1=keep[:, 0:1])
                 nc.vector.scalar_tensor_tensor(
-                    out=tile[:, 3, :],
-                    in0=tile[:, 3, :],
-                    scalar=keep[:, 0:1],
-                    in1=x_row_511[:, half * LOAD_COLS : (half + 1) * LOAD_COLS],
-                    op0=MULT,
-                    op1=ADD,
+                    out=tile[:, 3, span], in0=tile[:, 3, span], scalar=keep[:, 0:1], in1=x_row_511[:, row_span], op0=MULT, op1=ADD
                 )
             if c == 1:
-                nc.vector.tensor_scalar_mul(out=tile[:, 3, :], in0=tile[:, 3, :], scalar1=keep[:, 0:1])
+                nc.vector.tensor_scalar_mul(out=tile[:, 3, span], in0=tile[:, 3, span], scalar1=keep[:, 0:1])
 
         grouped_tiles = []
 
         def regroup(u):
             operand, c, col0, cols, v_cols = units[u]
-            first = col0 % LOAD_COLS
-            source = raw[(operand, c, col0 // LOAD_COLS)][:, :, first : first + cols]
+            raw_tile, offset = raw_at[(operand, c, col0)]
+            source = raw_tile[:, :, offset : offset + cols]
             grouped = grouped_pool.tile([P, cols, PACK], BF16, name="grouped", align_bytes=64)
             grouped_tiles.append(grouped)
             nc.vector.tensor_copy(
@@ -139,6 +128,8 @@ def tile_relativemultiheadattention_pa_kernel(tc, pos_embed, W_r, b_r, grad_out,
                     in_=source[:, :, v_cols:cols].rearrange("p j (c i) -> p c j i", i=RUN),
                 )
 
+        quantised = set()
+
         def quantise(u):
             operand, c, col0, cols, v_cols = units[u]
             nc.vector.quantize_mx(
@@ -146,12 +137,20 @@ def tile_relativemultiheadattention_pa_kernel(tc, pos_embed, W_r, b_r, grad_out,
                 scales=scales[operand][:, c, col0 : col0 + cols],
                 in_=grouped_tiles[u][:].rearrange("p w j -> p (w j)"),
             )
+            for offset in range(0, cols, M_TILE):
+                quantised.add((operand, c, col0 + offset))
 
         banks = {}
+        passes_done = {}
+        emptied = []
+        opened = []
 
         def one_pass(m, n, c):
-            if c == PASS_ORDER[0]:
+            if (m, n) not in banks:
                 banks[(m, n)] = psum_pool.tile([M_TILE, N_TILE], F32, name="bank")
+                passes_done[(m, n)] = []
+                opened.append((m, n))
+            passes_done[(m, n)].append(c)
             g_cols = slice(m * M_TILE, (m + 1) * M_TILE)
             x_cols = slice(n * N_TILE, (n + 1) * N_TILE)
             nc.tensor.matmul_mx(
@@ -160,9 +159,34 @@ def tile_relativemultiheadattention_pa_kernel(tc, pos_embed, W_r, b_r, grad_out,
                 lhsT_scale=scales["g"][:, c, g_cols],
                 rhs=codes["x"][:, c, x_cols].bitcast(E4M3_X4),
                 rhs_scale=scales["x"][:, c, x_cols],
-                start=(c == PASS_ORDER[0]),
-                stop=(c == PASS_ORDER[-1]),
+                start=(len(passes_done[(m, n)]) == 1),
+                stop=(len(passes_done[(m, n)]) == PASSES),
             )
+
+        groups = [
+            [(m, 0) for m in range(4)],
+            [(m, 1) for m in range(4)],
+            [(m, n) for n in range(N_TILES) for m in (4, 5)],
+            [(m, n) for n in range(N_TILES) for m in (6, 7)],
+        ]
+
+        def possible_passes():
+            for index, group in enumerate(groups):
+                if index >= 2 and not all([piece in emptied for piece in groups[index - 2]]):
+                    continue
+                if index == len(groups) - 1:
+                    if all([("g", c, m * M_TILE) in quantised for c in PASS_ORDER for m, n in group]):
+                        for m, n in group:
+                            for c in PASS_ORDER:
+                                if c not in passes_done.get((m, n), []):
+                                    one_pass(m, n, c)
+                    continue
+                for c in PASS_ORDER:
+                    for m, n in group:
+                        if c in passes_done.get((m, n), []):
+                            continue
+                        if ("g", c, m * M_TILE) in quantised and ("x", c, n * N_TILE + N_TILE - M_TILE) in quantised:
+                            one_pass(m, n, c)
 
         def empty(m, n, engine):
             result = result_pool.tile([M_TILE, N_TILE], F32, name="result")
@@ -173,41 +197,34 @@ def tile_relativemultiheadattention_pa_kernel(tc, pos_embed, W_r, b_r, grad_out,
             nc.sync.dma_start(
                 out=out[m * M_TILE : (m + 1) * M_TILE, n * N_TILE : (n + 1) * N_TILE], in_=result[:]
             )
+            emptied.append((m, n))
 
-        def matmuls_after(u):
-            operand, c, col0, cols, v_cols = units[u]
-            if u < first_part:
-                if operand == "x":
-                    for m in range(4):
-                        one_pass(m, col0 // N_TILE, c)
-            elif col0 == 512:
-                for n in range(N_TILES):
-                    for m in (4, 5):
-                        one_pass(m, n, c)
-            elif u == len(units) - 1:
-                for n in range(N_TILES):
-                    for m in (6, 7):
-                        for cc in PASS_ORDER:
-                            one_pass(m, n, cc)
-
+        quantised_units = []
         for u in range(len(units) + 1):
             if u < len(units):
                 operand, c, col0, cols, v_cols = units[u]
                 if operand == "x":
-                    mend_x(c, col0 // LOAD_COLS)
+                    mend_x(c, col0, cols)
                 regroup(u)
-            if u > 0:
+            if u > 0 and (u - 1) not in quantised_units:
                 quantise(u - 1)
-                matmuls_after(u - 1)
-            if u == first_part:
-                for m in range(4):
-                    empty(m, 0, "scalar")
-            if u == first_part + 1:
-                for m in range(4):
-                    empty(m, 1, "scalar")
+                quantised_units.append(u - 1)
+                possible_passes()
+            if shared_units - EAGER <= u < shared_units:
+                quantise(u)
+                quantised_units.append(u)
+                possible_passes()
+            if u == shared_units:
+                for piece in groups[0]:
+                    empty(piece[0], piece[1], "scalar")
+                possible_passes()
+            if u == shared_units + 1:
+                for piece in groups[1]:
+                    empty(piece[0], piece[1], "scalar")
+                possible_passes()
         empty(4, 0, "scalar")
-        empty(4, 1, "scalar")
         empty(5, 0, "vector")
+        empty(4, 1, "scalar")
         empty(5, 1, "vector")
         empty(6, 0, "scalar")
         empty(7, 0, "vector")

@@ -39,8 +39,10 @@ PASS_ORDER = (2, 1, 0)
 LOAD_PLAN = "x"
 FILL = False
 
-LOADS = [("g",2,0,512),("g",1,0,512),("g",0,0,512),("x",2,0,512),("x",2,512,512),("x",1,0,512),("x",1,512,512),("x",0,0,512),("x",0,512,512),("g",2,512,512),("g",1,512,512),("g",0,512,512)]
-UNITS = [("g",2,0,512,240),("g",1,0,512,240),("g",0,0,512,240),("x",2,0,512,240),("x",2,512,512,240),("x",1,0,512,208),("x",1,512,512,208),("x",0,0,512,176),("x",0,512,512,176),("g",2,512,256,256),("g",1,512,256,256),("g",0,512,256,256),("g",2,768,256,256),("g",1,768,256,256),("g",0,768,256,256)]
+LOADS = [("g",2,0,512),("x",2,0,512),("g",1,0,512),("x",2,512,512),("g",0,0,512),("x",1,0,512),("x",1,512,512),("x",0,0,512),("x",0,512,512),("g",2,512,512),("g",1,512,512),("g",0,512,512)]
+UNITS = [("g",2,0,512,240),("x",2,0,512,240),("g",1,0,512,240),("x",2,512,512,240),("g",0,0,512,240),("x",1,0,512,208),("x",1,512,512,208),("x",0,0,512,176),("x",0,512,512,176),("g",2,512,256,256),("g",1,512,256,256),("g",0,512,256,256),("g",2,768,256,256),("g",1,768,256,256),("g",0,768,256,256)]
+LAST_BY_PASS = 0
+TAIL = [(4,0,"scalar"),(5,0,"vector"),(4,1,"scalar"),(5,1,"vector"),(6,0,"scalar"),(7,0,"vector"),(6,1,"scalar"),(7,1,"vector")]
 
 FLOPS = 2 * TOKENS * D_OUT * D_IN
 BYTES = 2 * (TOKENS - 2) * D_IN + 2 * TOKENS * D_OUT + 4 * D_OUT * D_IN
@@ -82,19 +84,19 @@ def tile_relativemultiheadattention_pa_kernel(tc, pos_embed, W_r, b_r, grad_out,
 
         identity = const_pool.tile([P, P], F32, name="identity")
         make_identity(nc, identity[:])
+        x_row_511 = const_pool.tile([P, D_IN], BF16, name="x_row_511")
+        nc.vector.memset(x_row_511[:], 0.0)
         keep = const_pool.tile([P, 1], F32, name="keep")
         nc.vector.tensor_scalar(
             out=keep[:], in0=identity[:, P - 1 : P], scalar1=-1.0, scalar2=1.0, op0=MULT, op1=ADD
         )
-        x_row_511 = const_pool.tile([P, D_IN], BF16, name="x_row_511")
-        nc.vector.memset(x_row_511[:], 0.0)
 
         for raw_tile, (operand, c, col0, cols) in zip(raw_tiles, loads):
             if operand == "g":
                 rows = grad[c * K_PASS : (c + 1) * K_PASS, col0 : col0 + cols]
             else:
                 rows = pos[X_PASS_STARTS_AT_POS[c] : X_PASS_STARTS_AT_POS[c] + K_PASS, col0 : col0 + cols]
-            if (operand, c) == ("x", 0):
+            if (operand, c, col0) == ("x", PASS_ORDER[0], 0):
                 nc.sync.dma_start(out=x_row_511[P - 1 : P, :], in_=pos[512:513, :])
             nc.sync.dma_start(out=raw_tile[:], in_=rows.rearrange("(p j) w -> p j w", j=PACK))
 
@@ -175,6 +177,10 @@ def tile_relativemultiheadattention_pa_kernel(tc, pos_embed, W_r, b_r, grad_out,
                 if index >= 2 and not all([piece in emptied for piece in groups[index - 2]]):
                     continue
                 if index == len(groups) - 1:
+                    for c in PASS_ORDER[:LAST_BY_PASS]:
+                        for m, n in group:
+                            if c not in passes_done.get((m, n), []) and ("g", c, m * M_TILE) in quantised:
+                                one_pass(m, n, c)
                     if all([("g", c, m * M_TILE) in quantised for c in PASS_ORDER for m, n in group]):
                         for m, n in group:
                             for c in PASS_ORDER:
@@ -222,11 +228,5 @@ def tile_relativemultiheadattention_pa_kernel(tc, pos_embed, W_r, b_r, grad_out,
                 for piece in groups[1]:
                     empty(piece[0], piece[1], "scalar")
                 possible_passes()
-        empty(4, 0, "scalar")
-        empty(5, 0, "vector")
-        empty(4, 1, "scalar")
-        empty(5, 1, "vector")
-        empty(6, 0, "scalar")
-        empty(7, 0, "vector")
-        empty(6, 1, "scalar")
-        empty(7, 1, "vector")
+        for m, n, engine in TAIL:
+            empty(m, n, engine)

@@ -26,7 +26,7 @@ N_TILE = 512
 BANKS = 8
 N_TILES = D_IN // N_TILE
 
-RUN = 4
+RUN = 8
 GROUPED_BUFS = 4
 
 V_COLS_G = 240

@@ -1,8 +1,6 @@
 from contextlib import ExitStack
-
 import concourse.mybir as mybir
 from concourse.masks import make_identity
-
 BF16 = mybir.dt.bfloat16
 F32 = mybir.dt.float32
 U32 = mybir.dt.uint32
@@ -11,39 +9,105 @@ E4M3_X4 = mybir.dt.float8_e4m3fn_x4
 E5M2_X4 = mybir.dt.float8_e5m2_x4
 MULT = mybir.AluOpType.mult
 ADD = mybir.AluOpType.add
-
 P = 128
 PACK = 4
 K_PASS = P * PACK
-
 TOKENS = 1536
 D_OUT = 1024
 D_IN = 1024
 PASSES = TOKENS // K_PASS
-
 M_TILE = 128
 N_TILE = 512
-BANKS = 8
-N_TILES = D_IN // N_TILE
-
 RUN = 8
-GROUPED_BUFS = 4
-
-V_COLS_G = 240
-V_COLS_X = {}
-EAGER = 0
-
+GROUPED_BUFS = 6
 X_PASS_STARTS_AT_POS = (2, 513, 1024)
-PASS_ORDER = (2, 1, 0)
+PASS_ORDER = (0, 1, 2)
 
-LOAD_PLAN = "x"
-FILL = False
+def gl(c):
+    return ("g", c, 0, 512)
 
-LOADS = [("g",2,0,512),("x",2,0,512),("g",1,0,512),("x",2,512,512),("g",0,0,512),("x",1,0,512),("x",1,512,512),("x",0,0,512),("x",0,512,512),("g",2,512,512),("g",1,512,512),("g",0,512,512)]
-UNITS = [("g",2,0,512,240),("x",2,0,512,240),("g",1,0,512,240),("x",2,512,512,240),("g",0,0,512,240),("x",1,0,512,208),("x",1,512,512,208),("x",0,0,512,176),("x",0,512,512,176),("g",2,512,256,256),("g",1,512,256,256),("g",0,512,256,256),("g",2,768,256,256),("g",1,768,256,256),("g",0,768,256,256)]
-LAST_BY_PASS = 0
-TAIL = [(4,0,"scalar"),(5,0,"vector"),(4,1,"scalar"),(5,1,"vector"),(6,0,"scalar"),(7,0,"vector"),(6,1,"scalar"),(7,1,"vector")]
 
+def gr(c):
+    return ("g", c, 512, 512)
+
+
+def xl(c):
+    return ("x", c, 0, 512)
+
+
+def xr(c):
+    return ("x", c, 512, 512)
+
+
+def quarter(c, q):
+    return ("g", c, 256 * q, 256)
+
+
+def loads():
+    return [("fix", 0, 0, 0), gl(0), xl(0), ("fix", 1, 0, 0), gl(1), xr(0), gl(2), xl(1), xr(1), xl(2), xr(2), gr(0), gr(1), gr(2)]
+
+
+def rows(unit, v_cols):
+    operand, c, col0, cols = unit
+    both = [("v",) + unit + (0, v_cols)]
+    if v_cols < cols:
+        both.append(("c",) + unit + (v_cols, cols))
+    return both
+
+
+def q(unit):
+    return [("q",) + unit]
+
+
+def mend(c, col0):
+    return [("m", c, col0, 512)]
+
+
+def out_of(m, n, engine):
+    return [("e", m, n, engine), ("s", m, 512 * n, 512 * n + 512)]
+
+
+V_G = 240
+V_X0 = 224
+V_X = 240
+
+
+def steps():
+    return (
+    rows(gl(0), V_G)
+    + mend(0, 0) + rows(xl(0), V_X0) + q(gl(0))
+    + rows(gl(1), V_G) + q(xl(0))
+    + mend(0, 512) + rows(xr(0), V_X0) + q(gl(1))
+    + rows(gl(2), V_G) + mend(1, 0) + q(xr(0))
+    + rows(xl(1), V_X) + mend(1, 512) + q(gl(2))
+    + rows(xr(1), V_X) + q(xl(1))
+    + rows(xl(2), V_X) + q(xr(1))
+    + rows(xr(2), V_X) + q(xl(2))
+    + out_of(0, 0, "scalar") + rows(quarter(0, 2), 256) + q(xr(2)) + q(quarter(0, 2))
+    + out_of(1, 0, "scalar") + out_of(2, 0, "scalar") + out_of(3, 0, "scalar") + rows(quarter(1, 2), 256)
+    + out_of(0, 1, "scalar") + q(quarter(1, 2)) + out_of(1, 1, "scalar") + rows(quarter(2, 2), 256)
+    + out_of(2, 1, "scalar") + q(quarter(2, 2)) + out_of(3, 1, "scalar")
+    + rows(quarter(0, 3), 256) + q(quarter(0, 3)) + rows(quarter(1, 3), 256)
+    + out_of(4, 0, "scalar") + q(quarter(1, 3)) + rows(quarter(2, 3), 256) + out_of(4, 1, "scalar") + q(quarter(2, 3))
+    + out_of(5, 0, "scalar") + out_of(5, 1, "vector") + out_of(6, 0, "scalar") + out_of(6, 1, "vector")
+    + out_of(7, 0, "scalar") + out_of(7, 1, "vector")
+)
+GROUPS = [
+    [(m, 0) for m in range(4)],
+    [(m, 1) for m in range(4)],
+    [(4, 0), (4, 1), (5, 0), (5, 1)],
+    [(6, 0), (6, 1), (7, 0), (7, 1)],
+]
+
+
+def bank_of(m, n):
+    if m < 4:
+        return m + 4 * n
+    return 2 * (m - 4) + n
+
+
+PIECEWISE = 1
+LAST_BY_PASS = 1
 FLOPS = 2 * TOKENS * D_OUT * D_IN
 BYTES = 2 * (TOKENS - 2) * D_IN + 2 * TOKENS * D_OUT + 4 * D_OUT * D_IN
 
@@ -52,25 +116,23 @@ def tile_relativemultiheadattention_pa_kernel(tc, pos_embed, W_r, b_r, grad_out,
     nc = tc.nc
     pos = pos_embed.flatten_outer_dims()
     grad = grad_out.flatten_outer_dims()
-    loads = LOADS
-    units = UNITS
-    shared_units = len([unit for unit in units if unit[4] < unit[3]])
-
     with ExitStack() as stack:
         const_pool = stack.enter_context(tc.tile_pool(name="const", bufs=1))
         raw_pool = stack.enter_context(tc.tile_pool(name="raw", bufs=1))
         grouped_pool = stack.enter_context(tc.tile_pool(name="grouped", bufs=GROUPED_BUFS))
         mx_pool = stack.enter_context(tc.tile_pool(name="mx", bufs=1))
-        result_pool = stack.enter_context(tc.tile_pool(name="result", bufs=2 * BANKS))
-        psum_pool = stack.enter_context(tc.psum_pool(name="psum", bufs=BANKS))
+        result_pool = stack.enter_context(tc.tile_pool(name="result", bufs=1))
+        psum_pool = stack.enter_context(tc.psum_pool(name="psum", bufs=1))
         stack.enter_context(tc.manual_schedule())
-
         raw_at = {}
-        raw_tiles = []
-        for operand, c, col0, cols in loads:
+        load_tiles = {}
+        for load in loads():
+            operand, c, col0, cols = load
+            if operand == "fix":
+                continue
             raw_tile = raw_pool.tile([P, PACK, cols], BF16, name="raw_%s%d_%d" % (operand, c, col0))
-            raw_tiles.append(raw_tile)
-            for offset in range(0, cols, 256):
+            load_tiles[load] = raw_tile
+            for offset in range(0, cols, 128):
                 raw_at[(operand, c, col0 + offset)] = (raw_tile, offset)
         codes = {
             "g": mx_pool.tile([P, PASSES, D_OUT], U32, name="g_codes", align_bytes=64),
@@ -81,77 +143,75 @@ def tile_relativemultiheadattention_pa_kernel(tc, pos_embed, W_r, b_r, grad_out,
             "x": mx_pool.tile([P, PASSES, D_IN], U8, name="x_scales", align_bytes=64),
         }
         packed_dtype = {"g": E5M2_X4, "x": E4M3_X4}
-
-        identity = const_pool.tile([P, P], F32, name="identity")
+        identity = const_pool.tile([P, P], BF16, name="identity")
         make_identity(nc, identity[:])
-        x_row_511 = const_pool.tile([P, D_IN], BF16, name="x_row_511")
-        nc.vector.memset(x_row_511[:], 0.0)
+        fix = const_pool.tile([P, D_IN], BF16, name="fix")
         keep = const_pool.tile([P, 1], F32, name="keep")
         nc.vector.tensor_scalar(
             out=keep[:], in0=identity[:, P - 1 : P], scalar1=-1.0, scalar2=1.0, op0=MULT, op1=ADD
         )
-
-        for raw_tile, (operand, c, col0, cols) in zip(raw_tiles, loads):
+        for load in loads():
+            operand, c, col0, cols = load
+            if operand == "fix":
+                if c == 0:
+                    nc.sync.dma_start(out=fix[96:P, :], in_=pos[389:517, :].rearrange("(p j) w -> p j w", j=PACK)[:, 0, :])
+                else:
+                    nc.sync.dma_start(out=fix[P - 1 : P, :], in_=pos[512:513, :])
+                continue
             if operand == "g":
                 rows = grad[c * K_PASS : (c + 1) * K_PASS, col0 : col0 + cols]
             else:
                 rows = pos[X_PASS_STARTS_AT_POS[c] : X_PASS_STARTS_AT_POS[c] + K_PASS, col0 : col0 + cols]
-            if (operand, c, col0) == ("x", PASS_ORDER[0], 0):
-                nc.sync.dma_start(out=x_row_511[P - 1 : P, :], in_=pos[512:513, :])
-            nc.sync.dma_start(out=raw_tile[:], in_=rows.rearrange("(p j) w -> p j w", j=PACK))
+            nc.sync.dma_start(out=load_tiles[load][:], in_=rows.rearrange("(p j) w -> p j w", j=PACK))
 
         def mend_x(c, col0, cols):
             tile, offset = raw_at[("x", c, col0)]
             span = slice(offset, offset + cols)
-            row_span = slice(col0, col0 + cols)
             if c == 0:
                 nc.vector.tensor_scalar_mul(out=tile[:, 2, span], in0=tile[:, 2, span], scalar1=keep[:, 0:1])
-                nc.vector.scalar_tensor_tensor(
-                    out=tile[:, 3, span], in0=tile[:, 3, span], scalar=keep[:, 0:1], in1=x_row_511[:, row_span], op0=MULT, op1=ADD
-                )
+                nc.vector.tensor_copy(out=tile[96:P, 3, span], in_=fix[96:P, col0 : col0 + cols])
             if c == 1:
                 nc.vector.tensor_scalar_mul(out=tile[:, 3, span], in0=tile[:, 3, span], scalar1=keep[:, 0:1])
 
-        grouped_tiles = []
+        grouped_tiles = {}
 
-        def regroup(u):
-            operand, c, col0, cols, v_cols = units[u]
+        def grouped_of(operand, c, col0, cols):
+            key = (operand, c, col0, cols)
+            if key not in grouped_tiles:
+                grouped = grouped_pool.tile([P, cols, PACK], BF16, name="grouped", align_bytes=64)
+                grouped_tiles[key] = grouped
+            return grouped_tiles[key]
+
+        def strided(engine, operand, c, col0, cols, a, b):
             raw_tile, offset = raw_at[(operand, c, col0)]
-            source = raw_tile[:, :, offset : offset + cols]
-            grouped = grouped_pool.tile([P, cols, PACK], BF16, name="grouped", align_bytes=64)
-            grouped_tiles.append(grouped)
-            nc.vector.tensor_copy(
-                out=grouped[:, 0:v_cols, :].rearrange("p (c i) j -> p c j i", i=RUN),
-                in_=source[:, :, 0:v_cols].rearrange("p j (c i) -> p c j i", i=RUN),
-            )
-            if v_cols < cols:
-                nc.scalar.copy(
-                    out=grouped[:, v_cols:cols, :].rearrange("p (c i) j -> p c j i", i=RUN),
-                    in_=source[:, :, v_cols:cols].rearrange("p j (c i) -> p c j i", i=RUN),
-                )
+            source = raw_tile[:, :, offset + a : offset + b]
+            grouped = grouped_of(operand, c, col0, cols)
+            target = grouped[:, a:b, :].rearrange("p (c i) j -> p c j i", i=RUN)
+            if engine == "v":
+                nc.vector.tensor_copy(out=target, in_=source.rearrange("p j (c i) -> p c j i", i=RUN))
+            else:
+                nc.scalar.copy(out=target, in_=source.rearrange("p j (c i) -> p c j i", i=RUN))
 
         quantised = set()
 
-        def quantise(u):
-            operand, c, col0, cols, v_cols = units[u]
+        def quantise(operand, c, col0, cols):
             nc.vector.quantize_mx(
                 out=codes[operand][:, c, col0 : col0 + cols].bitcast(packed_dtype[operand]),
                 scales=scales[operand][:, c, col0 : col0 + cols],
-                in_=grouped_tiles[u][:].rearrange("p w j -> p (w j)"),
+                in_=grouped_tiles[(operand, c, col0, cols)][:].rearrange("p w j -> p (w j)"),
             )
             for offset in range(0, cols, M_TILE):
                 quantised.add((operand, c, col0 + offset))
 
         banks = {}
         passes_done = {}
-        emptied = []
-        opened = []
+        held = []
 
         def one_pass(m, n, c):
             if (m, n) not in banks:
-                banks[(m, n)] = psum_pool.tile([M_TILE, N_TILE], F32, name="bank")
+                banks[(m, n)] = psum_pool.tile([M_TILE, N_TILE], F32, name="bank%d" % bank_of(m, n))
                 passes_done[(m, n)] = []
-                opened.append((m, n))
+                held.append(bank_of(m, n))
             passes_done[(m, n)].append(c)
             g_cols = slice(m * M_TILE, (m + 1) * M_TILE)
             x_cols = slice(n * N_TILE, (n + 1) * N_TILE)
@@ -165,68 +225,54 @@ def tile_relativemultiheadattention_pa_kernel(tc, pos_embed, W_r, b_r, grad_out,
                 stop=(len(passes_done[(m, n)]) == PASSES),
             )
 
-        groups = [
-            [(m, 0) for m in range(4)],
-            [(m, 1) for m in range(4)],
-            [(m, n) for n in range(N_TILES) for m in (4, 5)],
-            [(m, n) for n in range(N_TILES) for m in (6, 7)],
-        ]
+        def may(m, n):
+            if (m, n) in banks:
+                return True
+            return bank_of(m, n) not in held
 
         def possible_passes():
-            for index, group in enumerate(groups):
-                if index >= 2 and not all([piece in emptied for piece in groups[index - 2]]):
-                    continue
-                if index == len(groups) - 1:
+            for index, group in enumerate(GROUPS):
+                if index >= len(GROUPS) - PIECEWISE:
                     for c in PASS_ORDER[:LAST_BY_PASS]:
                         for m, n in group:
-                            if c not in passes_done.get((m, n), []) and ("g", c, m * M_TILE) in quantised:
+                            if c not in passes_done.get((m, n), []) and may(m, n) and ("g", c, m * M_TILE) in quantised:
                                 one_pass(m, n, c)
-                    if all([("g", c, m * M_TILE) in quantised for c in PASS_ORDER for m, n in group]):
-                        for m, n in group:
+                    for m, n in group:
+                        if all([("g", c, m * M_TILE) in quantised and ("x", c, n * N_TILE + N_TILE - M_TILE) in quantised for c in PASS_ORDER]) and may(m, n):
                             for c in PASS_ORDER:
                                 if c not in passes_done.get((m, n), []):
                                     one_pass(m, n, c)
                     continue
                 for c in PASS_ORDER:
                     for m, n in group:
-                        if c in passes_done.get((m, n), []):
+                        if c in passes_done.get((m, n), []) or not may(m, n):
                             continue
                         if ("g", c, m * M_TILE) in quantised and ("x", c, n * N_TILE + N_TILE - M_TILE) in quantised:
                             one_pass(m, n, c)
 
-        def empty(m, n, engine):
-            result = result_pool.tile([M_TILE, N_TILE], F32, name="result")
-            if engine == "scalar":
-                nc.scalar.copy(out=result[:], in_=banks[(m, n)][:])
-            else:
-                nc.vector.tensor_copy(out=result[:], in_=banks[(m, n)][:])
-            nc.sync.dma_start(
-                out=out[m * M_TILE : (m + 1) * M_TILE, n * N_TILE : (n + 1) * N_TILE], in_=result[:]
-            )
-            emptied.append((m, n))
+        results = {}
 
-        quantised_units = []
-        for u in range(len(units) + 1):
-            if u < len(units):
-                operand, c, col0, cols, v_cols = units[u]
-                if operand == "x":
-                    mend_x(c, col0, cols)
-                regroup(u)
-            if u > 0 and (u - 1) not in quantised_units:
-                quantise(u - 1)
-                quantised_units.append(u - 1)
+        def empty(m, n, engine):
+            if m not in results:
+                results[m] = result_pool.tile([M_TILE, D_IN], F32, name="result%d" % m)
+            part = results[m][:, n * N_TILE : (n + 1) * N_TILE]
+            if engine == "scalar":
+                nc.scalar.copy(out=part, in_=banks[(m, n)][:])
+            else:
+                nc.vector.tensor_copy(out=part, in_=banks[(m, n)][:])
+            held.remove(bank_of(m, n))
+
+        for step in steps():
+            if step[0] == "v" or step[0] == "c":
+                strided("v" if step[0] == "v" else "s", step[1], step[2], step[3], step[4], step[5], step[6])
+            if step[0] == "q":
+                quantise(step[1], step[2], step[3], step[4])
                 possible_passes()
-            if shared_units - EAGER <= u < shared_units:
-                quantise(u)
-                quantised_units.append(u)
+            if step[0] == "m":
+                mend_x(step[1], step[2], step[3])
+            if step[0] == "e":
+                empty(step[1], step[2], step[3])
                 possible_passes()
-            if u == shared_units:
-                for piece in groups[0]:
-                    empty(piece[0], piece[1], "scalar")
-                possible_passes()
-            if u == shared_units + 1:
-                for piece in groups[1]:
-                    empty(piece[0], piece[1], "scalar")
-                possible_passes()
-        for m, n, engine in TAIL:
-            empty(m, n, engine)
+            if step[0] == "s":
+                m, c0, c1 = step[1:]
+                nc.sync.dma_start(out=out[m * M_TILE : (m + 1) * M_TILE, c0:c1], in_=results[m][:, c0:c1])

@@ -83,12 +83,12 @@ def steps():
     + rows(xr(1), V_X) + q(xl(1))
     + rows(xl(2), V_X) + q(xr(1))
     + rows(xr(2), V_X) + q(xl(2))
-    + out_of(0, 0, "scalar") + rows(quarter(0, 2), 256) + q(xr(2)) + q(quarter(0, 2))
-    + out_of(1, 0, "scalar") + out_of(2, 0, "scalar") + out_of(3, 0, "scalar") + rows(quarter(1, 2), 256)
-    + out_of(0, 1, "scalar") + q(quarter(1, 2)) + out_of(1, 1, "scalar") + rows(quarter(2, 2), 256)
-    + out_of(2, 1, "scalar") + q(quarter(2, 2)) + out_of(3, 1, "scalar")
-    + rows(quarter(0, 3), 256) + q(quarter(0, 3)) + rows(quarter(1, 3), 256)
-    + out_of(4, 0, "scalar") + q(quarter(1, 3)) + rows(quarter(2, 3), 256) + out_of(4, 1, "scalar") + q(quarter(2, 3))
+    + out_of(0, 0, "scalar") + rows(quarter(0, 2), 256) + q(xr(2))
+    + rows(quarter(1, 2), 256) + q(quarter(0, 2)) + out_of(1, 0, "scalar") + out_of(2, 0, "scalar") + out_of(3, 0, "scalar")
+    + rows(quarter(2, 2), 256) + q(quarter(1, 2)) + out_of(0, 1, "scalar") + out_of(1, 1, "scalar")
+    + rows(quarter(0, 3), 256) + q(quarter(2, 2)) + out_of(2, 1, "scalar") + out_of(3, 1, "scalar")
+    + rows(quarter(1, 3), 256) + q(quarter(0, 3)) + rows(quarter(2, 3), 256) + q(quarter(1, 3)) + q(quarter(2, 3))
+    + out_of(4, 0, "scalar") + out_of(4, 1, "scalar")
     + out_of(5, 0, "scalar") + out_of(5, 1, "vector") + out_of(6, 0, "scalar") + out_of(6, 1, "vector")
     + out_of(7, 0, "scalar") + out_of(7, 1, "vector")
 )

@@ -44,7 +44,7 @@ def quarter(c, q):
 
 
 def loads():
-    return [("fix", 0, 0, 0), gl(0), xl(0), ("fix", 1, 0, 0), gl(1), xr(0), gl(2), xl(1), xr(1), xl(2), xr(2), gr(0), gr(1), gr(2)]
+    return [("fix", 0, 0, 0), gl(0), xl(0), ("fix", 1, 0, 0), xr(0), gl(1), xl(1), xr(1), gl(2), xl(2), xr(2), gr(0), gr(1), gr(2)]
 
 
 def rows(unit, v_cols):
@@ -53,6 +53,18 @@ def rows(unit, v_cols):
     if v_cols < cols:
         both.append(("c",) + unit + (v_cols, cols))
     return both
+
+
+def tensor_rows(unit):
+    return [("p",) + unit + (T_FROM, T_TO)]
+
+
+def rows_with_tensor(unit):
+    return [("v",) + unit + (0, T_FROM), ("c",) + unit + (T_TO, 512), ("b",) + unit]
+
+
+def free_banks():
+    return [("f",)]
 
 
 def q(unit):
@@ -68,20 +80,22 @@ def out_of(m, n, engine):
 
 
 V_G = 240
-V_X0 = 224
 V_X = 240
+T_FROM = 160
+T_TO = 416
+T_BANKS = (4, 5)
 
 
 def steps():
     return (
     rows(gl(0), V_G)
-    + mend(0, 0) + rows(xl(0), V_X0) + q(gl(0))
-    + rows(gl(1), V_G) + q(xl(0))
-    + mend(0, 512) + rows(xr(0), V_X0) + q(gl(1))
-    + rows(gl(2), V_G) + mend(1, 0) + q(xr(0))
-    + rows(xl(1), V_X) + mend(1, 512) + q(gl(2))
-    + rows(xr(1), V_X) + q(xl(1))
-    + rows(xl(2), V_X) + q(xr(1))
+    + mend(0, 0) + rows(xl(0), V_X) + mend(0, 512) + q(gl(0))
+    + tensor_rows(gl(1)) + rows(xr(0), V_X) + q(xl(0))
+    + rows_with_tensor(gl(1)) + mend(1, 0) + q(xr(0))
+    + rows(xl(1), V_X) + mend(1, 512) + q(gl(1))
+    + tensor_rows(gl(2)) + rows(xr(1), V_X) + q(xl(1))
+    + rows_with_tensor(gl(2)) + free_banks() + q(xr(1))
+    + rows(xl(2), V_X) + q(gl(2))
     + rows(xr(2), V_X) + q(xl(2))
     + out_of(0, 0, "scalar") + rows(quarter(0, 2), 256) + q(xr(2))
     + rows(quarter(1, 2), 256) + q(quarter(0, 2)) + out_of(1, 0, "scalar") + out_of(2, 0, "scalar") + out_of(3, 0, "scalar")
@@ -192,6 +206,33 @@ def tile_relativemultiheadattention_pa_kernel(tc, pos_embed, W_r, b_r, grad_out,
             else:
                 nc.scalar.copy(out=target, in_=source.rearrange("p j (c i) -> p c j i", i=RUN))
 
+        tensor_parts = {}
+        parts_made = []
+        banks_free = []
+
+        def tensor_regroup(operand, c, col0, cols, a, b):
+            raw_tile, offset = raw_at[(operand, c, col0)]
+            tensor_parts[(operand, c, col0, cols)] = []
+            for at in range(a, b, 256):
+                n = min(256, b - at)
+                bank = psum_pool.tile([P, n, PACK], BF16, name="bank%d" % T_BANKS[len(parts_made) % len(T_BANKS)])
+                parts_made.append(1)
+                for k in range(0, n, 128):
+                    lo = offset + at + k
+                    nc.tensor.matmul(
+                        out=bank[:, k : k + 128, :].rearrange("p w j -> p j w"),
+                        lhsT=identity[:],
+                        rhs=raw_tile[:, :, lo : lo + 128],
+                        start=True,
+                        stop=True,
+                    )
+                tensor_parts[(operand, c, col0, cols)].append((bank, at, n))
+
+        def copy_parts(operand, c, col0, cols):
+            grouped = grouped_of(operand, c, col0, cols)
+            for bank, at, n in tensor_parts[(operand, c, col0, cols)]:
+                nc.scalar.copy(out=grouped[:, at : at + n, :], in_=bank[:])
+
         quantised = set()
 
         def quantise(operand, c, col0, cols):
@@ -228,7 +269,7 @@ def tile_relativemultiheadattention_pa_kernel(tc, pos_embed, W_r, b_r, grad_out,
         def may(m, n):
             if (m, n) in banks:
                 return True
-            return bank_of(m, n) not in held
+            return bank_of(m, n) not in held and (bank_of(m, n) not in T_BANKS or len(banks_free) > 0)
 
         def possible_passes():
             for index, group in enumerate(GROUPS):
@@ -265,6 +306,13 @@ def tile_relativemultiheadattention_pa_kernel(tc, pos_embed, W_r, b_r, grad_out,
         for step in steps():
             if step[0] == "v" or step[0] == "c":
                 strided("v" if step[0] == "v" else "s", step[1], step[2], step[3], step[4], step[5], step[6])
+            if step[0] == "p":
+                tensor_regroup(step[1], step[2], step[3], step[4], step[5], step[6])
+            if step[0] == "b":
+                copy_parts(step[1], step[2], step[3], step[4])
+            if step[0] == "f":
+                banks_free.append(1)
+                possible_passes()
             if step[0] == "q":
                 quantise(step[1], step[2], step[3], step[4])
                 possible_passes()

@@ -80,7 +80,8 @@ def out_of(m, n, engine):
 
 
 V_G = 240
-V_X = 240
+V_X0 = 208
+V_X = 224
 T_FROM = 160
 T_TO = 416
 T_BANKS = (4, 5)
@@ -89,8 +90,8 @@ T_BANKS = (4, 5)
 def steps():
     return (
     rows(gl(0), V_G)
-    + mend(0, 0) + rows(xl(0), V_X) + mend(0, 512) + q(gl(0))
-    + tensor_rows(gl(1)) + rows(xr(0), V_X) + q(xl(0))
+    + mend(0, 0) + rows(xl(0), V_X0) + mend(0, 512) + q(gl(0))
+    + tensor_rows(gl(1)) + rows(xr(0), V_X0) + q(xl(0))
     + rows_with_tensor(gl(1)) + mend(1, 0) + q(xr(0))
     + rows(xl(1), V_X) + mend(1, 512) + q(gl(1))
     + tensor_rows(gl(2)) + rows(xr(1), V_X) + q(xl(1))

from contextlib import ExitStack
import concourse.mybir as mybir
from concourse.masks import make_identity
BF16 = mybir.dt.bfloat16
F32 = mybir.dt.float32
U32 = mybir.dt.uint32
U8 = mybir.dt.uint8
E4M3_X4 = mybir.dt.float8_e4m3fn_x4
E5M2_X4 = mybir.dt.float8_e5m2_x4
MULT = mybir.AluOpType.mult
ADD = mybir.AluOpType.add
P = 128
PACK = 4
K_PASS = P * PACK
TOKENS = 1536
D_OUT = 1024
D_IN = 1024
PASSES = TOKENS // K_PASS
M_TILE = 128
N_TILE = 512
RUN = 8
GROUPED_BUFS = 6
X_PASS_STARTS_AT_POS = (2, 513, 1024)
PASS_ORDER = (0, 1, 2)

def gl(c):
    return ("g", c, 0, 512)


def gr(c):
    return ("g", c, 512, 512)


def xl(c):
    return ("x", c, 0, 512)


def xr(c):
    return ("x", c, 512, 512)


def quarter(c, q):
    return ("g", c, 256 * q, 256)


def loads():
    return [("fix", 0, 0, 0), gl(0), xl(0), ("fix", 1, 0, 0), xr(0), gl(1), xl(1), xr(1), gl(2), xl(2), xr(2), gr(0), gr(1), gr(2)]


def rows(unit, v_cols):
    operand, c, col0, cols = unit
    both = [("v",) + unit + (0, v_cols)]
    if v_cols < cols:
        both.append(("c",) + unit + (v_cols, cols))
    return both


def tensor_rows(unit):
    return [("p",) + unit + (T_FROM, T_TO)]


def rows_with_tensor(unit):
    return [("v",) + unit + (0, T_FROM), ("c",) + unit + (T_TO, 512), ("b",) + unit]


def free_banks():
    return [("f",)]


def q(unit):
    return [("q",) + unit]


def mend(c, col0):
    return [("m", c, col0, 512)]


def out_of(m, n, engine):
    return [("e", m, n, engine), ("s", m, 512 * n, 512 * n + 512)]


V_G = 240
V_X0 = 208
V_X = 224
T_FROM = 160
T_TO = 416
T_BANKS = (4, 5)


def steps():
    return (
    rows(gl(0), V_G)
    + mend(0, 0) + rows(xl(0), V_X0) + mend(0, 512) + q(gl(0))
    + tensor_rows(gl(1)) + rows(xr(0), V_X0) + q(xl(0))
    + rows_with_tensor(gl(1)) + mend(1, 0) + q(xr(0))
    + rows(xl(1), V_X) + mend(1, 512) + q(gl(1))
    + tensor_rows(gl(2)) + rows(xr(1), V_X) + q(xl(1))
    + rows_with_tensor(gl(2)) + free_banks() + q(xr(1))
    + rows(xl(2), V_X) + q(gl(2))
    + rows(xr(2), V_X) + q(xl(2))
    + out_of(0, 0, "scalar") + rows(quarter(0, 2), 256) + q(xr(2))
    + rows(quarter(1, 2), 256) + q(quarter(0, 2)) + out_of(1, 0, "scalar") + out_of(2, 0, "scalar") + out_of(3, 0, "scalar")
    + rows(quarter(2, 2), 256) + q(quarter(1, 2)) + out_of(0, 1, "scalar") + out_of(1, 1, "scalar")
    + rows(quarter(0, 3), 256) + q(quarter(2, 2)) + out_of(2, 1, "scalar") + out_of(3, 1, "scalar")
    + rows(quarter(1, 3), 256) + q(quarter(0, 3)) + rows(quarter(2, 3), 256) + q(quarter(1, 3)) + q(quarter(2, 3))
    + out_of(4, 0, "scalar") + out_of(4, 1, "scalar")
    + out_of(5, 0, "scalar") + out_of(5, 1, "vector") + out_of(6, 0, "scalar") + out_of(6, 1, "vector")
    + out_of(7, 0, "scalar") + out_of(7, 1, "vector")
)
GROUPS = [
    [(m, 0) for m in range(4)],
    [(m, 1) for m in range(4)],
    [(4, 0), (4, 1), (5, 0), (5, 1)],
    [(6, 0), (6, 1), (7, 0), (7, 1)],
]


def bank_of(m, n):
    if m < 4:
        return m + 4 * n
    return 2 * (m - 4) + n


PIECEWISE = 1
LAST_BY_PASS = 1
FLOPS = 2 * TOKENS * D_OUT * D_IN
BYTES = 2 * (TOKENS - 2) * D_IN + 2 * TOKENS * D_OUT + 4 * D_OUT * D_IN


def tile_relativemultiheadattention_pa_kernel(tc, pos_embed, W_r, b_r, grad_out, out):
    nc = tc.nc
    pos = pos_embed.flatten_outer_dims()
    grad = grad_out.flatten_outer_dims()
    with ExitStack() as stack:
        const_pool = stack.enter_context(tc.tile_pool(name="const", bufs=1))
        raw_pool = stack.enter_context(tc.tile_pool(name="raw", bufs=1))
        grouped_pool = stack.enter_context(tc.tile_pool(name="grouped", bufs=GROUPED_BUFS))
        mx_pool = stack.enter_context(tc.tile_pool(name="mx", bufs=1))
        result_pool = stack.enter_context(tc.tile_pool(name="result", bufs=1))
        psum_pool = stack.enter_context(tc.psum_pool(name="psum", bufs=1))
        stack.enter_context(tc.manual_schedule())
        raw_at = {}
        load_tiles = {}
        for load in loads():
            operand, c, col0, cols = load
            if operand == "fix":
                continue
            raw_tile = raw_pool.tile([P, PACK, cols], BF16, name="raw_%s%d_%d" % (operand, c, col0))
            load_tiles[load] = raw_tile
            for offset in range(0, cols, 128):
                raw_at[(operand, c, col0 + offset)] = (raw_tile, offset)
        codes = {
            "g": mx_pool.tile([P, PASSES, D_OUT], U32, name="g_codes", align_bytes=64),
            "x": mx_pool.tile([P, PASSES, D_IN], U32, name="x_codes", align_bytes=64),
        }
        scales = {
            "g": mx_pool.tile([P, PASSES, D_OUT], U8, name="g_scales", align_bytes=64),
            "x": mx_pool.tile([P, PASSES, D_IN], U8, name="x_scales", align_bytes=64),
        }
        packed_dtype = {"g": E5M2_X4, "x": E4M3_X4}
        identity = const_pool.tile([P, P], BF16, name="identity")
        make_identity(nc, identity[:])
        fix = const_pool.tile([P, D_IN], BF16, name="fix")
        keep = const_pool.tile([P, 1], F32, name="keep")
        nc.vector.tensor_scalar(
            out=keep[:], in0=identity[:, P - 1 : P], scalar1=-1.0, scalar2=1.0, op0=MULT, op1=ADD
        )
        for load in loads():
            operand, c, col0, cols = load
            if operand == "fix":
                if c == 0:
                    nc.sync.dma_start(out=fix[96:P, :], in_=pos[389:517, :].rearrange("(p j) w -> p j w", j=PACK)[:, 0, :])
                else:
                    nc.sync.dma_start(out=fix[P - 1 : P, :], in_=pos[512:513, :])
                continue
            if operand == "g":
                rows = grad[c * K_PASS : (c + 1) * K_PASS, col0 : col0 + cols]
            else:
                rows = pos[X_PASS_STARTS_AT_POS[c] : X_PASS_STARTS_AT_POS[c] + K_PASS, col0 : col0 + cols]
            nc.sync.dma_start(out=load_tiles[load][:], in_=rows.rearrange("(p j) w -> p j w", j=PACK))

        def mend_x(c, col0, cols):
            tile, offset = raw_at[("x", c, col0)]
            span = slice(offset, offset + cols)
            if c == 0:
                nc.vector.tensor_scalar_mul(out=tile[:, 2, span], in0=tile[:, 2, span], scalar1=keep[:, 0:1])
                nc.vector.tensor_copy(out=tile[96:P, 3, span], in_=fix[96:P, col0 : col0 + cols])
            if c == 1:
                nc.vector.tensor_scalar_mul(out=tile[:, 3, span], in0=tile[:, 3, span], scalar1=keep[:, 0:1])

        grouped_tiles = {}

        def grouped_of(operand, c, col0, cols):
            key = (operand, c, col0, cols)
            if key not in grouped_tiles:
                grouped = grouped_pool.tile([P, cols, PACK], BF16, name="grouped", align_bytes=64)
                grouped_tiles[key] = grouped
            return grouped_tiles[key]

        def strided(engine, operand, c, col0, cols, a, b):
            raw_tile, offset = raw_at[(operand, c, col0)]
            source = raw_tile[:, :, offset + a : offset + b]
            grouped = grouped_of(operand, c, col0, cols)
            target = grouped[:, a:b, :].rearrange("p (c i) j -> p c j i", i=RUN)
            if engine == "v":
                nc.vector.tensor_copy(out=target, in_=source.rearrange("p j (c i) -> p c j i", i=RUN))
            else:
                nc.scalar.copy(out=target, in_=source.rearrange("p j (c i) -> p c j i", i=RUN))

        tensor_parts = {}
        parts_made = []
        banks_free = []

        def tensor_regroup(operand, c, col0, cols, a, b):
            raw_tile, offset = raw_at[(operand, c, col0)]
            tensor_parts[(operand, c, col0, cols)] = []
            for at in range(a, b, 256):
                n = min(256, b - at)
                bank = psum_pool.tile([P, n, PACK], BF16, name="bank%d" % T_BANKS[len(parts_made) % len(T_BANKS)])
                parts_made.append(1)
                for k in range(0, n, 128):
                    lo = offset + at + k
                    nc.tensor.matmul(
                        out=bank[:, k : k + 128, :].rearrange("p w j -> p j w"),
                        lhsT=identity[:],
                        rhs=raw_tile[:, :, lo : lo + 128],
                        start=True,
                        stop=True,
                    )
                tensor_parts[(operand, c, col0, cols)].append((bank, at, n))

        def copy_parts(operand, c, col0, cols):
            grouped = grouped_of(operand, c, col0, cols)
            for bank, at, n in tensor_parts[(operand, c, col0, cols)]:
                nc.scalar.copy(out=grouped[:, at : at + n, :], in_=bank[:])

        quantised = set()

        def quantise(operand, c, col0, cols):
            nc.vector.quantize_mx(
                out=codes[operand][:, c, col0 : col0 + cols].bitcast(packed_dtype[operand]),
                scales=scales[operand][:, c, col0 : col0 + cols],
                in_=grouped_tiles[(operand, c, col0, cols)][:].rearrange("p w j -> p (w j)"),
            )
            for offset in range(0, cols, M_TILE):
                quantised.add((operand, c, col0 + offset))

        banks = {}
        passes_done = {}
        held = []

        def one_pass(m, n, c):
            if (m, n) not in banks:
                banks[(m, n)] = psum_pool.tile([M_TILE, N_TILE], F32, name="bank%d" % bank_of(m, n))
                passes_done[(m, n)] = []
                held.append(bank_of(m, n))
            passes_done[(m, n)].append(c)
            g_cols = slice(m * M_TILE, (m + 1) * M_TILE)
            x_cols = slice(n * N_TILE, (n + 1) * N_TILE)
            nc.tensor.matmul_mx(
                out=banks[(m, n)][:],
                lhsT=codes["g"][:, c, g_cols].bitcast(E5M2_X4),
                lhsT_scale=scales["g"][:, c, g_cols],
                rhs=codes["x"][:, c, x_cols].bitcast(E4M3_X4),
                rhs_scale=scales["x"][:, c, x_cols],
                start=(len(passes_done[(m, n)]) == 1),
                stop=(len(passes_done[(m, n)]) == PASSES),
            )

        def may(m, n):
            if (m, n) in banks:
                return True
            return bank_of(m, n) not in held and (bank_of(m, n) not in T_BANKS or len(banks_free) > 0)

        def possible_passes():
            for index, group in enumerate(GROUPS):
                if index >= len(GROUPS) - PIECEWISE:
                    for c in PASS_ORDER[:LAST_BY_PASS]:
                        for m, n in group:
                            if c not in passes_done.get((m, n), []) and may(m, n) and ("g", c, m * M_TILE) in quantised:
                                one_pass(m, n, c)
                    for m, n in group:
                        if all([("g", c, m * M_TILE) in quantised and ("x", c, n * N_TILE + N_TILE - M_TILE) in quantised for c in PASS_ORDER]) and may(m, n):
                            for c in PASS_ORDER:
                                if c not in passes_done.get((m, n), []):
                                    one_pass(m, n, c)
                    continue
                for c in PASS_ORDER:
                    for m, n in group:
                        if c in passes_done.get((m, n), []) or not may(m, n):
                            continue
                        if ("g", c, m * M_TILE) in quantised and ("x", c, n * N_TILE + N_TILE - M_TILE) in quantised:
                            one_pass(m, n, c)

        results = {}

        def empty(m, n, engine):
            if m not in results:
                results[m] = result_pool.tile([M_TILE, D_IN], F32, name="result%d" % m)
            part = results[m][:, n * N_TILE : (n + 1) * N_TILE]
            if engine == "scalar":
                nc.scalar.copy(out=part, in_=banks[(m, n)][:])
            else:
                nc.vector.tensor_copy(out=part, in_=banks[(m, n)][:])
            held.remove(bank_of(m, n))

        for step in steps():
            if step[0] == "v" or step[0] == "c":
                strided("v" if step[0] == "v" else "s", step[1], step[2], step[3], step[4], step[5], step[6])
            if step[0] == "p":
                tensor_regroup(step[1], step[2], step[3], step[4], step[5], step[6])
            if step[0] == "b":
                copy_parts(step[1], step[2], step[3], step[4])
            if step[0] == "f":
                banks_free.append(1)
                possible_passes()
            if step[0] == "q":
                quantise(step[1], step[2], step[3], step[4])
                possible_passes()
            if step[0] == "m":
                mend_x(step[1], step[2], step[3])
            if step[0] == "e":
                empty(step[1], step[2], step[3])
                possible_passes()
            if step[0] == "s":
                m, c0, c1 = step[1:]
                nc.sync.dma_start(out=out[m * M_TILE : (m + 1) * M_TILE, c0:c1], in_=results[m][:, c0:c1])
